import numpy as np
import ml_dtypes


def mxq(x, axis, fmt="e4m3"):
    dtype, down = {"e4m3": (ml_dtypes.float8_e4m3fn, 7), "e5m2": (ml_dtypes.float8_e5m2, 14)}[fmt]
    v = np.moveaxis(np.asarray(x, np.float32).astype(ml_dtypes.bfloat16).astype(np.float64), axis, -1)
    blocks = v.reshape(v.shape[:-1] + (-1, 32))
    amax = np.abs(blocks).max(-1, keepdims=True)
    byte = np.maximum(np.where(amax > 0, np.frexp(amax)[1] - 1 + 127, 0) - down, 1)
    scale = np.exp2(byte - 127.0)
    codes = (blocks / scale).astype(np.float32).astype(dtype).astype(np.float64)
    return np.moveaxis((codes * scale).reshape(v.shape), -1, axis)


WIDE = False


def mx_kscale(k):
    if not WIDE:
        return np.ones(k)
    levels = np.array([10, -10, 5, -5, 0])
    a = np.random.permutation(np.resize(levels, k // 512 * 4)).reshape(k // 512, 4)
    idx = np.arange(k)
    return np.exp2(a[idx // 512, idx % 128 // 32])


BF16 = ml_dtypes.bfloat16


def bf(x):
    return np.asarray(x, np.float32).astype(BF16)


def f64(x):
    return np.asarray(x).astype(np.float64)


E2M1 = np.array([0.0, 0.5, 1.0, 1.5, 2.0, 3.0, 4.0, 6.0, -0.0, -0.5, -1.0, -1.5, -2.0, -3.0, -4.0, -6.0])


def pack_weight(w, fmt):
    k, n = w.shape
    w = f64(bf(w)).reshape(k // 32, 32, n)
    amax = np.abs(w).max(1)
    if fmt == "e4m3":
        byte = np.frexp(amax)[1] - 1 + 127 - 7
    else:
        mant, ex = np.frexp(amax / 6.0)
        byte = np.where(mant > 0.5, ex, ex - 1) + 127
    byte = np.clip(np.where(amax > 0, byte, 1), 1, 254)
    scaled = (w * np.exp2(127.0 - byte)[:, None, :]).reshape(k, n).astype(np.float32)
    by_word = np.ascontiguousarray(scaled.reshape(k // 512, 128, 4, n).transpose(0, 1, 3, 2))
    if fmt == "e4m3":
        words = by_word.astype(ml_dtypes.float8_e4m3fn).view(np.uint8)
    else:
        c = by_word.astype(ml_dtypes.float4_e2m1fn).view(np.uint8) & 0xF
        words = c[..., 0::2] | (c[..., 1::2] << 4)
    return np.ascontiguousarray(words), np.ascontiguousarray(byte.astype(np.uint8).reshape(k // 512, 16, n))


def unpack_weight(words, scales, fmt):
    g, p, n, _ = words.shape
    if fmt == "e4m3":
        vals = np.ascontiguousarray(words).view(ml_dtypes.float8_e4m3fn).astype(np.float64)
    else:
        nib = np.empty((g, p, n, 4), np.uint8)
        nib[..., 0::2] = words & 0xF
        nib[..., 1::2] = words >> 4
        vals = E2M1[nib]
    vals = vals * np.repeat(np.exp2(scales.astype(np.float64) - 127.0), 8, axis=1)[..., None]
    return vals.transpose(0, 1, 3, 2).reshape(g * 512, n)


B, N, IN_DIM, OUT_DIM, NUM_F = 2, 256, 1024, 768, 8


def silu(v):
    return v / (1.0 + np.exp(-v))


def setup_inputs():
    t = mx_kscale(IN_DIM)
    x = bf(np.random.standard_normal((B, N, IN_DIM)))
    base_weight_words, base_weight_scales = pack_weight((np.random.standard_normal((OUT_DIM, IN_DIM)) / np.sqrt(IN_DIM)).T, "e4m3")
    return {"x": x,
            "base_weight_words": base_weight_words,
            "base_weight_scales": base_weight_scales,
            "grid": bf(np.arange(NUM_F) + 1.0),
            "scale_sp": bf(1.0 + 0.1 * np.random.standard_normal(OUT_DIM)),
            "coef": bf(np.random.uniform(size=(IN_DIM, NUM_F)) * t[:, None]),
            "conv_w": bf(np.random.standard_normal((NUM_F, OUT_DIM, IN_DIM)) / np.sqrt(IN_DIM) / t[None, None, :]),
            "conv_b": bf(np.random.standard_normal((NUM_F, OUT_DIM)) * 0.1)}


def reference(x, base_weight_words, base_weight_scales, grid, scale_sp, coef, conv_w, conv_b):
    x = f64(x)
    b, n, d = x.shape
    xf = x.reshape(b * n, d)
    base_out = mxq(silu(xf), 1, "e4m3") @ unpack_weight(base_weight_words, base_weight_scales, "e4m3")
    s = np.sin(xf[:, None, :] * f64(grid)[None, :, None]) * f64(coef).T[None, :, :]
    sq = mxq(s, 2, "e4m3")
    wq = mxq(f64(conv_w), 2, "e4m3")
    spline = np.matmul(sq.transpose(1, 0, 2), wq.transpose(0, 2, 1)).transpose(1, 0, 2) + f64(conv_b)[None, :, :]
    out = base_out + spline.sum(axis=1) * f64(scale_sp)
    return out.reshape(b, n, OUT_DIM)

@@ -1,0 +1,303 @@
+import math
+from contextlib import ExitStack
+
+import concourse.mybir as mybir
+from concourse.masks import make_identity
+
+F32 = mybir.dt.float32
+BF16 = mybir.dt.bfloat16
+I32 = mybir.dt.int32
+U32 = mybir.dt.uint32
+U8 = mybir.dt.uint8
+FP8X4 = mybir.dt.float8_e4m3fn_x4
+ALU = mybir.AluOpType
+ACT = mybir.ActivationFunctionType
+
+P = 128
+PACK = 4
+K_PASS = P * PACK
+TOKENS = 512
+IN_DIM = 1024
+OUT_DIM = 768
+NUM_F = 8
+PASSES = IN_DIM // K_PASS
+O_TILES = OUT_DIM // P
+TOK_TILES = TOKENS // P
+WORDS = K_PASS // 2
+HALF = TOKENS // 2
+UNIT = TOKENS * PACK
+UNITS = NUM_F * PASSES
+AHEAD = 2
+ANGLES_AHEAD = 4
+W_BUFS = 2
+
+FLOPS = 2 * TOKENS * IN_DIM * OUT_DIM * (NUM_F + 1)
+
+
+def tile_efficient_skan_batch_kernel(
+    tc, x, base_weight_words, base_weight_scales, grid, scale_sp, coef, conv_w, conv_b, out
+):
+    nc = tc.nc
+    xf = x.flatten_outer_dims()
+    outf = out.flatten_outer_dims()
+
+    with ExitStack() as ctx:
+        const = ctx.enter_context(tc.tile_pool(name="const", bufs=1))
+        wpool = ctx.enter_context(tc.tile_pool(name="wpool", bufs=W_BUFS))
+        two = ctx.enter_context(tc.tile_pool(name="two", bufs=2))
+        three = ctx.enter_context(tc.tile_pool(name="three", bufs=3))
+        four = ctx.enter_context(tc.tile_pool(name="four", bufs=ANGLES_AHEAD))
+        psum_acc = ctx.enter_context(tc.psum_pool(name="psum_acc", bufs=1))
+        psum_tp = ctx.enter_context(tc.psum_pool(name="psum_tp", bufs=2))
+        ctx.enter_context(tc.manual_schedule())
+
+        x_sb = const.tile([P, TOK_TILES, IN_DIM], BF16)
+        x_view = xf.rearrange("(i p) k -> p i k", p=P)
+        for h in range(2):
+            nc.sync.dma_start(out=x_sb[:, 2 * h : 2 * h + 2, :], in_=x_view[:, 2 * h : 2 * h + 2, :])
+
+        grid_bc = const.tile([P, NUM_F], BF16)
+        nc.scalar.dma_start(out=grid_bc[:], in_=grid.partition_broadcast(P))
+        coef_sb = const.tile([P, PASSES, PACK, NUM_F], BF16)
+        nc.scalar.dma_start(
+            out=coef_sb[:].rearrange("p g t f -> p g (t f)"),
+            in_=coef.rearrange("(g p t) f -> p g (t f)", g=PASSES, t=PACK),
+        )
+        rows = const.tile([P, P], BF16)
+        nc.vector.memset(rows[:], 0.0)
+        nc.scalar.dma_start(out=rows[0 : NUM_F * O_TILES, :], in_=conv_b.rearrange("f (j c) -> (f j) c", c=P))
+        nc.scalar.dma_start(out=rows[64 : 64 + O_TILES, :], in_=scale_sp.rearrange("(j c) -> j c", c=P))
+
+        base_codes = const.tile([P, PASSES, OUT_DIM], U32, align_bytes=64)
+        nc.sync.dma_start(
+            out=base_codes[:].bitcast(I32),
+            in_=base_weight_words.rearrange("g p n t -> p g (n t)").bitcast(I32),
+        )
+        base_scales = const.tile([P, PASSES, OUT_DIM], U8, align_bytes=64)
+        nc.vector.memset(base_scales[:].bitcast(I32), 0)
+        for q in range(4):
+            nc.sync.dma_start(
+                out=base_scales[32 * q : 32 * q + 4, :, :].bitcast(I32),
+                in_=base_weight_scales[:, 4 * q : 4 * q + 4, :].rearrange("g r n -> r g n").bitcast(I32),
+            )
+
+        w_raw = {}
+
+        def load_weights(f):
+            w_raw[f] = wpool.tile([P, O_TILES, IN_DIM], BF16, name="w_raw", tag="w_raw")
+            nc.sync.dma_start(out=w_raw[f][:], in_=conv_w[f].rearrange("(j p) k -> p j k", p=P))
+
+        for f in range(W_BUFS):
+            load_weights(f)
+
+        ident_f32 = const.tile([P, P], F32)
+        make_identity(nc, ident_f32[:])
+        ident_bf = const.tile([P, P], BF16)
+        make_identity(nc, ident_bf[:])
+
+        turns = const.tile([P, NUM_F], F32)
+        coef_t = const.tile([P, NUM_F, PASSES, PACK], F32)
+        x_t = const.tile([P, PASSES, TOKENS, PACK], BF16)
+        whole = {}
+        frac = {}
+        sine = {}
+        s_bf = {}
+        s_codes = {}
+        s_scales = {}
+        w_bf = {}
+        w_codes = {}
+        w_scales = {}
+        acc = [
+            psum_acc.tile([P, TOKENS], F32, tag="acc%d" % j, name="acc%d" % j) for j in range(O_TILES)
+        ]
+
+        def whole_turns(u):
+            f, g = divmod(u, PASSES)
+            whole[u] = two.tile([P, UNIT], I32, name="whole", tag="whole")
+            nc.vector.tensor_scalar(
+                out=whole[u][:],
+                in0=x_t[:, g, :, :].rearrange("p w t -> p (w t)"),
+                scalar1=turns[:, f : f + 1],
+                scalar2=None,
+                op0=ALU.mult,
+            )
+
+        def reduce_angle(u):
+            f, g = divmod(u, PASSES)
+            frac[u] = four.tile([P, UNIT], F32, name="frac", tag="frac")
+            nc.vector.scalar_tensor_tensor(
+                out=frac[u][:],
+                in0=x_t[:, g, :, :].rearrange("p w t -> p (w t)"),
+                scalar=turns[:, f : f + 1],
+                in1=whole[u][:],
+                op0=ALU.mult,
+                op1=ALU.subtract,
+            )
+
+        def sine_of(u):
+            sine[u] = three.tile([P, UNIT], F32, name="sine", tag="sine")
+            nc.scalar.activation(out=sine[u][:], in_=frac[u][:], func=ACT.Sin, scale=2.0 * math.pi)
+
+        def basis(u):
+            f, g = divmod(u, PASSES)
+            s_bf[u] = two.tile([P, TOKENS, PACK], BF16, align_bytes=64, name="s_bf", tag="s_bf")
+            nc.vector.tensor_tensor(
+                out=s_bf[u][:],
+                in0=sine[u][:].rearrange("p (w t) -> p w t", t=PACK),
+                in1=coef_t[:, f, g, :].unsqueeze(1).to_broadcast([P, TOKENS, PACK]),
+                op=ALU.mult,
+            )
+
+        def quantise_basis(u):
+            s_codes[u] = three.tile([P, TOKENS], U32, align_bytes=64, name="s_codes", tag="s_codes")
+            s_scales[u] = three.tile([P, TOKENS], U8, align_bytes=64, name="s_scales", tag="s_scales")
+            nc.vector.quantize_mx(
+                out=s_codes[u][:].bitcast(FP8X4),
+                scales=s_scales[u][:],
+                in_=s_bf[u][:].rearrange("p w t -> p (w t)"),
+            )
+
+        def transpose_weights(u):
+            f, g = divmod(u, PASSES)
+            w_bf[u] = three.tile([P, O_TILES, P, PACK], BF16, align_bytes=64, name="w_bf", tag="w_bf")
+            for jj in range(O_TILES // 2):
+                wt_ps = psum_tp.tile([P, 2, 2, P], F32, tag="tp", name="wt_ps")
+                for a in range(2):
+                    for e in range(2):
+                        nc.tensor.transpose(
+                            wt_ps[:, a, e, :],
+                            w_raw[f][:, 2 * jj + a, :].bitcast(F32)[:, WORDS * g + e : WORDS * (g + 1) : 2],
+                            ident_f32[:],
+                        )
+                nc.scalar.copy(
+                    out=w_bf[u][:, 2 * jj : 2 * jj + 2, :, :].bitcast(F32),
+                    in_=wt_ps[:].rearrange("p a e o -> p a o e"),
+                )
+            if g == PASSES - 1 and f + W_BUFS < NUM_F:
+                load_weights(f + W_BUFS)
+
+        def quantise_weights(u):
+            w_codes[u] = three.tile([P, O_TILES, P], U32, align_bytes=64, name="w_codes", tag="w_codes")
+            w_scales[u] = three.tile([P, O_TILES, P], U8, align_bytes=64, name="w_scales", tag="w_scales")
+            for lo, hi in ((0, 4), (4, 6)):
+                nc.vector.quantize_mx(
+                    out=w_codes[u][:, lo:hi, :].rearrange("p j o -> p (j o)").bitcast(FP8X4),
+                    scales=w_scales[u][:, lo:hi, :].rearrange("p j o -> p (j o)"),
+                    in_=w_bf[u][:, lo:hi, :, :].rearrange("p j o t -> p (j o t)"),
+                )
+
+        def multiply(u):
+            for j in range(O_TILES):
+                nc.tensor.matmul_mx(
+                    out=acc[j][:],
+                    lhsT=w_codes[u][:, j, :].bitcast(FP8X4),
+                    lhsT_scale=w_scales[u][:, j, :],
+                    rhs=s_codes[u][:].bitcast(FP8X4),
+                    rhs_scale=s_scales[u][:],
+                    start=(u == 0),
+                    stop=(u == UNITS - 1),
+                )
+
+        nc.vector.tensor_scalar(
+            out=turns[:], in0=grid_bc[:], scalar1=1.0 / (2.0 * math.pi), scalar2=None, op0=ALU.mult
+        )
+        for g in range(PASSES):
+            for h in range(2):
+                xt_ps = psum_tp.tile([P, 2, HALF], F32, tag="tp", name="xt_ps")
+                for e in range(2):
+                    for i in range(2):
+                        nc.tensor.transpose(
+                            xt_ps[:, e, P * i : P * (i + 1)],
+                            x_sb[:, 2 * h + i, :].bitcast(F32)[:, WORDS * g + e : WORDS * (g + 1) : 2],
+                            ident_f32[:],
+                        )
+                nc.vector.tensor_copy(
+                    out=x_t[:, g, HALF * h : HALF * (h + 1), :].bitcast(F32),
+                    in_=xt_ps[:].rearrange("p e w -> p w e"),
+                )
+            whole_turns(g)
+        for u in range(ANGLES_AHEAD):
+            reduce_angle(u)
+            if u + PASSES <= ANGLES_AHEAD:
+                whole_turns(u + PASSES)
+
+        silu = const.tile([P, PASSES, UNIT], BF16, align_bytes=64)
+        silu_codes = const.tile([P, PASSES, TOKENS], U32, align_bytes=64)
+        silu_scales = const.tile([P, PASSES, TOKENS], U8, align_bytes=64)
+        for g in range(PASSES):
+            nc.scalar.activation(
+                out=silu[:, g, :], in_=x_t[:, g, :, :].rearrange("p w t -> p (w t)"), func=ACT.Silu
+            )
+        for u in range(AHEAD):
+            sine_of(u)
+        for u in range(AHEAD):
+            transpose_weights(u)
+
+        nc.vector.tensor_copy(out=coef_t[:], in_=coef_sb[:].rearrange("p g t f -> p f g t"))
+        rows_ps = psum_tp.tile([P, P], BF16, tag="tp")
+        nc.tensor.transpose(rows_ps[:], rows[:], ident_bf[:])
+        cols = const.tile([P, P], F32)
+        nc.vector.tensor_copy(out=cols[:], in_=rows_ps[:])
+        gain = cols[:, 64 : 64 + O_TILES]
+        bias = const.tile([P, O_TILES], F32)
+        nc.vector.tensor_reduce(
+            out=bias[:],
+            in_=cols[:, 0 : NUM_F * O_TILES].rearrange("p (f j) -> p j f", j=O_TILES),
+            axis=mybir.AxisListType.X,
+            op=ALU.add,
+        )
+        nc.vector.tensor_mul(out=bias[:], in0=bias[:], in1=gain)
+        for g in range(PASSES):
+            nc.vector.quantize_mx(
+                out=silu_codes[:, g, :].bitcast(FP8X4), scales=silu_scales[:, g, :], in_=silu[:, g, :]
+            )
+
+        base_sb = const.tile([P, O_TILES, TOKENS], F32)
+        for j in range(O_TILES):
+            o_cols = slice(P * j, P * (j + 1))
+            base_ps = psum_tp.tile([P, TOKENS], F32, tag="tp", name="base_ps")
+            for g in range(PASSES):
+                nc.tensor.matmul_mx(
+                    out=base_ps[:],
+                    lhsT=base_codes[:, g, o_cols].bitcast(FP8X4),
+                    lhsT_scale=base_scales[:, g, o_cols],
+                    rhs=silu_codes[:, g, :].bitcast(FP8X4),
+                    rhs_scale=silu_scales[:, g, :],
+                    start=(g == 0),
+                    stop=(g == PASSES - 1),
+                )
+            nc.scalar.activation(
+                out=base_sb[:, j, :], in_=base_ps[:], func=ACT.Identity, bias=bias[:, j : j + 1], scale=1.0
+            )
+
+        for u in range(UNITS):
+            ahead = u + AHEAD
+            quantise_weights(u)
+            basis(u)
+            if u + ANGLES_AHEAD < UNITS:
+                reduce_angle(u + ANGLES_AHEAD)
+            quantise_basis(u)
+            if u + ANGLES_AHEAD + 1 < UNITS:
+                whole_turns(u + ANGLES_AHEAD + 1)
+            if ahead < UNITS:
+                transpose_weights(ahead)
+                sine_of(ahead)
+            multiply(u)
+
+        out_view = outf.rearrange("(i p) o -> p i o", p=P)
+        for j in range(O_TILES):
+            out_t = two.tile([P, TOKENS], F32, name="out_t", tag="out_t")
+            nc.vector.scalar_tensor_tensor(
+                out=out_t[:],
+                in0=acc[j][:],
+                scalar=gain[:, j : j + 1],
+                in1=base_sb[:, j, :],
+                op0=ALU.mult,
+                op1=ALU.add,
+            )
+            back_ps = psum_tp.tile([P, TOK_TILES, P], F32, tag="tp", name="back_ps")
+            for i in range(TOK_TILES):
+                nc.tensor.transpose(back_ps[:, i, :], out_t[:, P * i : P * (i + 1)], ident_f32[:])
+            out_sb = two.tile([P, TOK_TILES, P], F32, name="out_sb", tag="out_sb")
+            nc.scalar.copy(out=out_sb[:], in_=back_ps[:])
+            nc.sync.dma_start(out=out_view[:, :, P * j : P * (j + 1)], in_=out_sb[:])

@@ -30,6 +30,7 @@ UNITS = NUM_F * PASSES
 AHEAD = 2
 ANGLES_AHEAD = 4
 W_BUFS = 2
+PAIRS = O_TILES // 2
 
 FLOPS = 2 * TOKENS * IN_DIM * OUT_DIM * (NUM_F + 1)
 
@@ -48,13 +49,15 @@ def tile_efficient_skan_batch_kernel(
         three = ctx.enter_context(tc.tile_pool(name="three", bufs=3))
         four = ctx.enter_context(tc.tile_pool(name="four", bufs=ANGLES_AHEAD))
         psum_acc = ctx.enter_context(tc.psum_pool(name="psum_acc", bufs=1))
-        psum_tp = ctx.enter_context(tc.psum_pool(name="psum_tp", bufs=2))
+        psum_tp = ctx.enter_context(tc.psum_pool(name="psum_tp", bufs=1))
+        psum_coef = ctx.enter_context(tc.psum_pool(name="psum_coef", bufs=1))
         ctx.enter_context(tc.manual_schedule())
 
         x_sb = const.tile([P, TOK_TILES, IN_DIM], BF16)
         x_view = xf.rearrange("(i p) k -> p i k", p=P)
-        for h in range(2):
-            nc.sync.dma_start(out=x_sb[:, 2 * h : 2 * h + 2, :], in_=x_view[:, 2 * h : 2 * h + 2, :])
+        for g in range(PASSES):
+            k_cols = slice(K_PASS * g, K_PASS * (g + 1))
+            nc.sync.dma_start(out=x_sb[:, :, k_cols], in_=x_view[:, :, k_cols])
 
         grid_bc = const.tile([P, NUM_F], BF16)
         nc.scalar.dma_start(out=grid_bc[:], in_=grid.partition_broadcast(P))
@@ -68,6 +71,13 @@ def tile_efficient_skan_batch_kernel(
         nc.scalar.dma_start(out=rows[0 : NUM_F * O_TILES, :], in_=conv_b.rearrange("f (j c) -> (f j) c", c=P))
         nc.scalar.dma_start(out=rows[64 : 64 + O_TILES, :], in_=scale_sp.rearrange("(j c) -> j c", c=P))
 
+        w_raw = {}
+
+        def load_weights(f):
+            w_raw[f] = wpool.tile([P, O_TILES, IN_DIM], BF16, name="w_raw", tag="w_raw")
+            nc.sync.dma_start(out=w_raw[f][:], in_=conv_w[f].rearrange("(j p) k -> p j k", p=P))
+
+        load_weights(0)
         base_codes = const.tile([P, PASSES, OUT_DIM], U32, align_bytes=64)
         nc.sync.dma_start(
             out=base_codes[:].bitcast(I32),
@@ -80,14 +90,7 @@ def tile_efficient_skan_batch_kernel(
                 out=base_scales[32 * q : 32 * q + 4, :, :].bitcast(I32),
                 in_=base_weight_scales[:, 4 * q : 4 * q + 4, :].rearrange("g r n -> r g n").bitcast(I32),
             )
-
-        w_raw = {}
-
-        def load_weights(f):
-            w_raw[f] = wpool.tile([P, O_TILES, IN_DIM], BF16, name="w_raw", tag="w_raw")
-            nc.sync.dma_start(out=w_raw[f][:], in_=conv_w[f].rearrange("(j p) k -> p j k", p=P))
-
-        for f in range(W_BUFS):
+        for f in range(1, W_BUFS):
             load_weights(f)
 
         ident_f32 = const.tile([P, P], F32)
@@ -96,7 +99,7 @@ def tile_efficient_skan_batch_kernel(
         make_identity(nc, ident_bf[:])
 
         turns = const.tile([P, NUM_F], F32)
-        coef_t = const.tile([P, NUM_F, PASSES, PACK], F32)
+        coef_ps = psum_coef.tile([P, PASSES, PACK, NUM_F], F32)
         x_t = const.tile([P, PASSES, TOKENS, PACK], BF16)
         whole = {}
         frac = {}
@@ -107,19 +110,18 @@ def tile_efficient_skan_batch_kernel(
         w_bf = {}
         w_codes = {}
         w_scales = {}
-        acc = [
-            psum_acc.tile([P, TOKENS], F32, tag="acc%d" % j, name="acc%d" % j) for j in range(O_TILES)
-        ]
+        acc = []
 
-        def whole_turns(u):
+        def whole_turns(engine, u):
             f, g = divmod(u, PASSES)
-            whole[u] = two.tile([P, UNIT], I32, name="whole", tag="whole")
-            nc.vector.tensor_scalar(
+            whole[u] = three.tile([P, UNIT], I32, name="whole", tag="whole")
+            engine.tensor_scalar(
                 out=whole[u][:],
                 in0=x_t[:, g, :, :].rearrange("p w t -> p (w t)"),
                 scalar1=turns[:, f : f + 1],
-                scalar2=None,
+                scalar2=0.0,
                 op0=ALU.mult,
+                op1=ALU.add,
             )
 
         def reduce_angle(u):
@@ -134,17 +136,13 @@ def tile_efficient_skan_batch_kernel(
                 op1=ALU.subtract,
             )
 
-        def sine_of(u):
-            sine[u] = three.tile([P, UNIT], F32, name="sine", tag="sine")
-            nc.scalar.activation(out=sine[u][:], in_=frac[u][:], func=ACT.Sin, scale=2.0 * math.pi)
-
         def basis(u):
             f, g = divmod(u, PASSES)
             s_bf[u] = two.tile([P, TOKENS, PACK], BF16, align_bytes=64, name="s_bf", tag="s_bf")
             nc.vector.tensor_tensor(
                 out=s_bf[u][:],
                 in0=sine[u][:].rearrange("p (w t) -> p w t", t=PACK),
-                in1=coef_t[:, f, g, :].unsqueeze(1).to_broadcast([P, TOKENS, PACK]),
+                in1=coef_ps[:, g, :, f].unsqueeze(1).to_broadcast([P, TOKENS, PACK]),
                 op=ALU.mult,
             )
 
@@ -157,25 +155,6 @@ def tile_efficient_skan_batch_kernel(
                 in_=s_bf[u][:].rearrange("p w t -> p (w t)"),
             )
 
-        def transpose_weights(u):
-            f, g = divmod(u, PASSES)
-            w_bf[u] = three.tile([P, O_TILES, P, PACK], BF16, align_bytes=64, name="w_bf", tag="w_bf")
-            for jj in range(O_TILES // 2):
-                wt_ps = psum_tp.tile([P, 2, 2, P], F32, tag="tp", name="wt_ps")
-                for a in range(2):
-                    for e in range(2):
-                        nc.tensor.transpose(
-                            wt_ps[:, a, e, :],
-                            w_raw[f][:, 2 * jj + a, :].bitcast(F32)[:, WORDS * g + e : WORDS * (g + 1) : 2],
-                            ident_f32[:],
-                        )
-                nc.scalar.copy(
-                    out=w_bf[u][:, 2 * jj : 2 * jj + 2, :, :].bitcast(F32),
-                    in_=wt_ps[:].rearrange("p a e o -> p a o e"),
-                )
-            if g == PASSES - 1 and f + W_BUFS < NUM_F:
-                load_weights(f + W_BUFS)
-
         def quantise_weights(u):
             w_codes[u] = three.tile([P, O_TILES, P], U32, align_bytes=64, name="w_codes", tag="w_codes")
             w_scales[u] = three.tile([P, O_TILES, P], U8, align_bytes=64, name="w_scales", tag="w_scales")
@@ -186,24 +165,53 @@ def tile_efficient_skan_batch_kernel(
                     in_=w_bf[u][:, lo:hi, :, :].rearrange("p j o t -> p (j o t)"),
                 )
 
-        def multiply(u):
-            for j in range(O_TILES):
-                nc.tensor.matmul_mx(
-                    out=acc[j][:],
-                    lhsT=w_codes[u][:, j, :].bitcast(FP8X4),
-                    lhsT_scale=w_scales[u][:, j, :],
-                    rhs=s_codes[u][:].bitcast(FP8X4),
-                    rhs_scale=s_scales[u][:],
-                    start=(u == 0),
-                    stop=(u == UNITS - 1),
-                )
+        def multiply(u, j):
+            nc.tensor.matmul_mx(
+                out=acc[j][:],
+                lhsT=w_codes[u][:, j, :].bitcast(FP8X4),
+                lhsT_scale=w_scales[u][:, j, :],
+                rhs=s_codes[u][:].bitcast(FP8X4),
+                rhs_scale=s_scales[u][:],
+                start=(u == 0),
+                stop=(u == UNITS - 1),
+            )
+
+        def tensor_and_scalar_round(new, old):
+            if new is not None:
+                f, g = divmod(new, PASSES)
+                w_bf[new] = three.tile([P, O_TILES, P, PACK], BF16, align_bytes=64, name="w_bf", tag="w_bf")
+                sine[new] = three.tile([P, UNIT], F32, name="sine", tag="sine")
+            for jj in range(PAIRS):
+                if new is not None:
+                    wt_ps = psum_tp.tile([P, 2, 2, P], F32, tag="tp", name="wt_ps")
+                    for a in range(2):
+                        for e in range(2):
+                            nc.tensor.transpose(
+                                wt_ps[:, a, e, :],
+                                w_raw[f][:, 2 * jj + a, :].bitcast(F32)[:, WORDS * g + e : WORDS * (g + 1) : 2],
+                                ident_f32[:],
+                            )
+                    nc.scalar.copy(
+                        out=w_bf[new][:, 2 * jj : 2 * jj + 2, :, :].bitcast(F32),
+                        in_=wt_ps[:].rearrange("p a e o -> p a o e"),
+                    )
+                    if jj < 2:
+                        half = slice(UNIT // 2 * jj, UNIT // 2 * (jj + 1))
+                        nc.scalar.activation(
+                            out=sine[new][:, half], in_=frac[new][:, half], func=ACT.Sin, scale=2.0 * math.pi
+                        )
+                if old is not None:
+                    multiply(old, 2 * jj)
+                    multiply(old, 2 * jj + 1)
+            if new is not None and g == PASSES - 1 and f + W_BUFS < NUM_F:
+                load_weights(f + W_BUFS)
 
         nc.vector.tensor_scalar(
             out=turns[:], in0=grid_bc[:], scalar1=1.0 / (2.0 * math.pi), scalar2=None, op0=ALU.mult
         )
         for g in range(PASSES):
             for h in range(2):
-                xt_ps = psum_tp.tile([P, 2, HALF], F32, tag="tp", name="xt_ps")
+                xt_ps = psum_acc.tile([P, 2, HALF], F32, tag="acc%d" % (2 * g + h), name="xt_ps")
                 for e in range(2):
                     for i in range(2):
                         nc.tensor.transpose(
@@ -215,11 +223,13 @@ def tile_efficient_skan_batch_kernel(
                     out=x_t[:, g, HALF * h : HALF * (h + 1), :].bitcast(F32),
                     in_=xt_ps[:].rearrange("p e w -> p w e"),
                 )
-            whole_turns(g)
+            whole_turns(nc.vector, g)
         for u in range(ANGLES_AHEAD):
             reduce_angle(u)
-            if u + PASSES <= ANGLES_AHEAD:
-                whole_turns(u + PASSES)
+            if u + PASSES < ANGLES_AHEAD:
+                whole_turns(nc.vector, u + PASSES)
+        for u in range(ANGLES_AHEAD, ANGLES_AHEAD + 2):
+            whole_turns(nc.gpsimd, u)
 
         silu = const.tile([P, PASSES, UNIT], BF16, align_bytes=64)
         silu_codes = const.tile([P, PASSES, TOKENS], U32, align_bytes=64)
@@ -228,14 +238,18 @@ def tile_efficient_skan_batch_kernel(
             nc.scalar.activation(
                 out=silu[:, g, :], in_=x_t[:, g, :, :].rearrange("p w t -> p (w t)"), func=ACT.Silu
             )
-        for u in range(AHEAD):
-            sine_of(u)
-        for u in range(AHEAD):
-            transpose_weights(u)
-
-        nc.vector.tensor_copy(out=coef_t[:], in_=coef_sb[:].rearrange("p g t f -> p f g t"))
-        rows_ps = psum_tp.tile([P, P], BF16, tag="tp")
+        rows_ps = psum_acc.tile([P, P], BF16, tag="acc4")
         nc.tensor.transpose(rows_ps[:], rows[:], ident_bf[:])
+        nc.tensor.matmul(
+            out=coef_ps[:].rearrange("p g t f -> p (g t f)"),
+            lhsT=ident_bf[:],
+            rhs=coef_sb[:].rearrange("p g t f -> p (g t f)"),
+            start=True,
+            stop=True,
+        )
+        for u in range(AHEAD):
+            tensor_and_scalar_round(u, None)
+
         cols = const.tile([P, P], F32)
         nc.vector.tensor_copy(out=cols[:], in_=rows_ps[:])
         gain = cols[:, 64 : 64 + O_TILES]
@@ -255,7 +269,7 @@ def tile_efficient_skan_batch_kernel(
         base_sb = const.tile([P, O_TILES, TOKENS], F32)
         for j in range(O_TILES):
             o_cols = slice(P * j, P * (j + 1))
-            base_ps = psum_tp.tile([P, TOKENS], F32, tag="tp", name="base_ps")
+            base_ps = psum_acc.tile([P, TOKENS], F32, tag="acc%d" % j, name="base_ps")
             for g in range(PASSES):
                 nc.tensor.matmul_mx(
                     out=base_ps[:],
@@ -269,20 +283,19 @@ def tile_efficient_skan_batch_kernel(
             nc.scalar.activation(
                 out=base_sb[:, j, :], in_=base_ps[:], func=ACT.Identity, bias=bias[:, j : j + 1], scale=1.0
             )
+        for j in range(O_TILES):
+            acc.append(psum_acc.tile([P, TOKENS], F32, tag="acc%d" % j, name="acc%d" % j))
 
         for u in range(UNITS):
-            ahead = u + AHEAD
             quantise_weights(u)
             basis(u)
             if u + ANGLES_AHEAD < UNITS:
                 reduce_angle(u + ANGLES_AHEAD)
             quantise_basis(u)
-            if u + ANGLES_AHEAD + 1 < UNITS:
-                whole_turns(u + ANGLES_AHEAD + 1)
-            if ahead < UNITS:
-                transpose_weights(ahead)
-                sine_of(ahead)
-            multiply(u)
+            if u + ANGLES_AHEAD + 2 < UNITS:
+                whole_turns(nc.gpsimd, u + ANGLES_AHEAD + 2)
+            tensor_and_scalar_round(u + AHEAD if u + AHEAD < UNITS else None, u - 1 if u > 0 else None)
+        tensor_and_scalar_round(None, UNITS - 1)
 
         out_view = outf.rearrange("(i p) o -> p i o", p=P)
         for j in range(O_TILES):
@@ -295,7 +308,7 @@ def tile_efficient_skan_batch_kernel(
                 op0=ALU.mult,
                 op1=ALU.add,
             )
-            back_ps = psum_tp.tile([P, TOK_TILES, P], F32, tag="tp", name="back_ps")
+            back_ps = psum_acc.tile([P, TOK_TILES, P], F32, tag="acc%d" % j, name="back_ps")
             for i in range(TOK_TILES):
                 nc.tensor.transpose(back_ps[:, i, :], out_t[:, P * i : P * (i + 1)], ident_f32[:])
             out_sb = two.tile([P, TOK_TILES, P], F32, name="out_sb", tag="out_sb")

@@ -22,15 +22,20 @@ OUT_DIM = 768
 NUM_F = 8
 PASSES = IN_DIM // K_PASS
 O_TILES = OUT_DIM // P
-TOK_TILES = TOKENS // P
+SWEEPS = 2
+SWEEP = TOKENS // SWEEPS
+S_TILES = SWEEP // P
 WORDS = K_PASS // 2
-HALF = TOKENS // 2
-UNIT = TOKENS * PACK
-UNITS = NUM_F * PASSES
-AHEAD = 2
-ANGLES_AHEAD = 4
-W_BUFS = 2
-PAIRS = O_TILES // 2
+STEP = SWEEP * PACK
+UNITS = PASSES * NUM_F
+STEPS = SWEEPS * UNITS
+WEIGHTS_AHEAD = 2
+TENSOR_AHEAD = 2
+SINES_AHEAD = 3
+ANGLES_AHEAD = 5
+TURNS_AHEAD = 7
+CHUNKS = ((0, 512), (512, 768))
+BANK = 512
 
 FLOPS = 2 * TOKENS * IN_DIM * OUT_DIM * (NUM_F + 1)
 
@@ -44,21 +49,33 @@ def tile_efficient_skan_batch_kernel(
 
     with ExitStack() as ctx:
         const = ctx.enter_context(tc.tile_pool(name="const", bufs=1))
-        wpool = ctx.enter_context(tc.tile_pool(name="wpool", bufs=W_BUFS))
+        wpool = ctx.enter_context(tc.tile_pool(name="wpool", bufs=4))
         two = ctx.enter_context(tc.tile_pool(name="two", bufs=2))
         three = ctx.enter_context(tc.tile_pool(name="three", bufs=3))
-        four = ctx.enter_context(tc.tile_pool(name="four", bufs=ANGLES_AHEAD))
-        psum_acc = ctx.enter_context(tc.psum_pool(name="psum_acc", bufs=1))
-        psum_tp = ctx.enter_context(tc.psum_pool(name="psum_tp", bufs=1))
-        psum_coef = ctx.enter_context(tc.psum_pool(name="psum_coef", bufs=1))
+        five = ctx.enter_context(tc.tile_pool(name="five", bufs=5))
+        four = ctx.enter_context(tc.tile_pool(name="four", bufs=4))
+        psum = ctx.enter_context(tc.psum_pool(name="psum", bufs=1))
+        psum_work = ctx.enter_context(tc.psum_pool(name="psum_work", bufs=2))
         ctx.enter_context(tc.manual_schedule())
 
-        x_sb = const.tile([P, TOK_TILES, IN_DIM], BF16)
+        x_sb = const.tile([P, SWEEPS * S_TILES, IN_DIM], BF16)
         x_view = xf.rearrange("(i p) k -> p i k", p=P)
-        for g in range(PASSES):
-            k_cols = slice(K_PASS * g, K_PASS * (g + 1))
-            nc.sync.dma_start(out=x_sb[:, :, k_cols], in_=x_view[:, :, k_cols])
+        w_raw = {}
 
+        def load_x(h, g):
+            tiles = slice(S_TILES * h, S_TILES * (h + 1))
+            k_cols = slice(K_PASS * g, K_PASS * (g + 1))
+            nc.sync.dma_start(out=x_sb[:, tiles, k_cols], in_=x_view[:, tiles, k_cols])
+
+        def load_weights(u):
+            g, f = divmod(u, NUM_F)
+            w_raw[u] = wpool.tile([P, O_TILES, K_PASS], BF16, name="w_raw", tag="w_raw")
+            nc.sync.dma_start(
+                out=w_raw[u][:],
+                in_=conv_w[f, :, K_PASS * g : K_PASS * (g + 1)].rearrange("(j p) k -> p j k", p=P),
+            )
+
+        load_x(0, 0)
         grid_bc = const.tile([P, NUM_F], BF16)
         nc.scalar.dma_start(out=grid_bc[:], in_=grid.partition_broadcast(P))
         coef_sb = const.tile([P, PASSES, PACK, NUM_F], BF16)
@@ -66,180 +83,303 @@ def tile_efficient_skan_batch_kernel(
             out=coef_sb[:].rearrange("p g t f -> p g (t f)"),
             in_=coef.rearrange("(g p t) f -> p g (t f)", g=PASSES, t=PACK),
         )
-        rows = const.tile([P, P], BF16)
-        nc.vector.memset(rows[:], 0.0)
-        nc.scalar.dma_start(out=rows[0 : NUM_F * O_TILES, :], in_=conv_b.rearrange("f (j c) -> (f j) c", c=P))
-        nc.scalar.dma_start(out=rows[64 : 64 + O_TILES, :], in_=scale_sp.rearrange("(j c) -> j c", c=P))
-
-        w_raw = {}
-
-        def load_weights(f):
-            w_raw[f] = wpool.tile([P, O_TILES, IN_DIM], BF16, name="w_raw", tag="w_raw")
-            nc.sync.dma_start(out=w_raw[f][:], in_=conv_w[f].rearrange("(j p) k -> p j k", p=P))
-
         load_weights(0)
+        load_x(0, 1)
+        load_weights(1)
+        load_x(1, 0)
+        load_x(1, 1)
+        load_weights(2)
         base_codes = const.tile([P, PASSES, OUT_DIM], U32, align_bytes=64)
-        nc.sync.dma_start(
-            out=base_codes[:].bitcast(I32),
-            in_=base_weight_words.rearrange("g p n t -> p g (n t)").bitcast(I32),
-        )
         base_scales = const.tile([P, PASSES, OUT_DIM], U8, align_bytes=64)
-        nc.vector.memset(base_scales[:].bitcast(I32), 0)
-        for q in range(4):
+        load_weights(3)
+
+        def load_base():
             nc.sync.dma_start(
-                out=base_scales[32 * q : 32 * q + 4, :, :].bitcast(I32),
-                in_=base_weight_scales[:, 4 * q : 4 * q + 4, :].rearrange("g r n -> r g n").bitcast(I32),
+                out=base_codes[:].bitcast(I32),
+                in_=base_weight_words.rearrange("g p n t -> p g (n t)").bitcast(I32),
             )
-        for f in range(1, W_BUFS):
-            load_weights(f)
+            for q in range(4):
+                nc.sync.dma_start(
+                    out=base_scales[32 * q : 32 * q + 4, :, :].bitcast(I32),
+                    in_=base_weight_scales[:, 4 * q : 4 * q + 4, :].rearrange("g r n -> r g n").bitcast(I32),
+                )
 
         ident_f32 = const.tile([P, P], F32)
         make_identity(nc, ident_f32[:])
         ident_bf = const.tile([P, P], BF16)
         make_identity(nc, ident_bf[:])
+        ones_bf = const.tile([P, P], BF16)
+        nc.vector.memset(ones_bf[:], 1.0)
+        nc.vector.memset(base_scales[:].bitcast(I32), 0)
+        rows = const.tile([P, 2, OUT_DIM], BF16)
+        nc.gpsimd.memset(rows[:], 0.0)
+        nc.sync.dma_start(out=rows[0:NUM_F, 0, :], in_=conv_b)
+        nc.sync.dma_start(out=rows[0:1, 1, :], in_=scale_sp.rearrange("(a o) -> a o", a=1))
 
         turns = const.tile([P, NUM_F], F32)
-        coef_ps = psum_coef.tile([P, PASSES, PACK, NUM_F], F32)
-        x_t = const.tile([P, PASSES, TOKENS, PACK], BF16)
+        coef_ps = psum.tile([P, PASSES, PACK, NUM_F], F32, tag="coef")
+        w_codes = const.tile([P, UNITS, OUT_DIM], U32, align_bytes=64)
+        w_scales = const.tile([P, UNITS, OUT_DIM], U8, align_bytes=64)
+        base_sb = const.tile([P, SWEEPS * S_TILES, OUT_DIM], F32)
+        gain_bc = const.tile([P, OUT_DIM], F32)
+        bias_bc = const.tile([P, OUT_DIM], F32)
+        x_ps = {}
+        x_t = {}
         whole = {}
         frac = {}
         sine = {}
         s_bf = {}
+        diag = {}
         s_codes = {}
         s_scales = {}
         w_bf = {}
-        w_codes = {}
-        w_scales = {}
-        acc = []
+        silu = {}
+        silu_codes = {}
+        silu_scales = {}
+        acc = {}
 
-        def whole_turns(engine, u):
-            f, g = divmod(u, PASSES)
-            whole[u] = three.tile([P, UNIT], I32, name="whole", tag="whole")
+        def where(v):
+            h, u = divmod(v, UNITS)
+            g, f = divmod(u, NUM_F)
+            return h, u, g, f
+
+        def transpose_x(h, g, bank):
+            for e in range(2):
+                for i in range(S_TILES):
+                    nc.tensor.transpose(
+                        bank[:, e, P * i : P * (i + 1)],
+                        x_sb[:, S_TILES * h + i, :].bitcast(F32)[:, WORDS * g + e : WORDS * (g + 1) : 2],
+                        ident_f32[:],
+                    )
+
+        def x_to_psum(h, g):
+            x_ps[h, g] = psum.tile([P, 2, SWEEP], F32, tag="x", name="x_ps")
+            transpose_x(h, g, x_ps[h, g])
+
+        def x_to_sbuf(h, g, bank):
+            x_t[h, g] = const.tile([P, 2, SWEEP], F32, name="x_t_%d%d" % (h, g))
+            nc.scalar.copy(out=x_t[h, g][:], in_=bank[:])
+
+        def whole_turns(engine, v):
+            h, u, g, f = where(v)
+            whole[v] = four.tile([P, STEP], I32, name="whole", tag="whole")
             engine.tensor_scalar(
-                out=whole[u][:],
-                in0=x_t[:, g, :, :].rearrange("p w t -> p (w t)"),
+                out=whole[v][:],
+                in0=x_t[h, g][:].rearrange("p e w -> p (e w)").bitcast(BF16),
                 scalar1=turns[:, f : f + 1],
                 scalar2=0.0,
                 op0=ALU.mult,
                 op1=ALU.add,
             )
 
-        def reduce_angle(u):
-            f, g = divmod(u, PASSES)
-            frac[u] = four.tile([P, UNIT], F32, name="frac", tag="frac")
+        def reduce_angle(v):
+            h, u, g, f = where(v)
+            frac[v] = five.tile([P, STEP], F32, name="frac", tag="frac")
             nc.vector.scalar_tensor_tensor(
-                out=frac[u][:],
-                in0=x_t[:, g, :, :].rearrange("p w t -> p (w t)"),
+                out=frac[v][:],
+                in0=x_ps[h, g][:].rearrange("p e w -> p (e w)").bitcast(BF16),
                 scalar=turns[:, f : f + 1],
-                in1=whole[u][:],
+                in1=whole[v][:],
                 op0=ALU.mult,
                 op1=ALU.subtract,
             )
 
-        def basis(u):
-            f, g = divmod(u, PASSES)
-            s_bf[u] = two.tile([P, TOKENS, PACK], BF16, align_bytes=64, name="s_bf", tag="s_bf")
+        def take_sine(v):
+            sine[v] = four.tile([P, STEP], F32, name="sine", tag="sine")
+            if by_tensor(v):
+                nc.scalar.activation(
+                    out=sine[v][:].rearrange("p (e s w) -> p e s w", e=2, s=2),
+                    in_=frac[v][:].rearrange("p (e w s) -> p e s w", e=2, s=2),
+                    func=ACT.Sin,
+                    scale=2.0 * math.pi,
+                )
+            else:
+                nc.scalar.activation(out=sine[v][:], in_=frac[v][:], func=ACT.Sin, scale=2.0 * math.pi)
+
+        def by_tensor(v):
+            return v >= UNITS and v % 3 == 1
+
+        def make_diagonals(v):
+            h, u, g, f = where(v)
+            diag[v] = two.tile([P, PACK, P], F32, name="diag", tag="diag")
+            for t in range(PACK):
+                nc.gpsimd.tensor_scalar(
+                    out=diag[v][:, t, :],
+                    in0=ident_f32[:],
+                    scalar1=coef_sb[:, g, t, f : f + 1],
+                    scalar2=0.0,
+                    op0=ALU.mult,
+                    op1=ALU.add,
+                )
+
+        def basis_by_tensor(v, i):
+            if i == 0:
+                s_bf[v] = four.tile([P, SWEEP, PACK], BF16, align_bytes=64, name="s_bf", tag="s_bf")
+            bank = psum_work.tile([P, PACK, P], F32, tag="work", name="s_ps")
+            for t in range(PACK):
+                nc.tensor.matmul(
+                    out=bank[:, t, :],
+                    lhsT=diag[v][:, t, :],
+                    rhs=sine[v][:, SWEEP * t + P * i : SWEEP * t + P * (i + 1)],
+                    start=True,
+                    stop=True,
+                )
+            nc.scalar.copy(
+                out=s_bf[v][:, P * i : P * (i + 1), :], in_=bank[:].rearrange("p t w -> p w t")
+            )
+
+        def basis(v):
+            h, u, g, f = where(v)
+            s_bf[v] = four.tile([P, SWEEP, PACK], BF16, align_bytes=64, name="s_bf", tag="s_bf")
             nc.vector.tensor_tensor(
-                out=s_bf[u][:],
-                in0=sine[u][:].rearrange("p (w t) -> p w t", t=PACK),
-                in1=coef_ps[:, g, :, f].unsqueeze(1).to_broadcast([P, TOKENS, PACK]),
+                out=s_bf[v][:].rearrange("p w (e s) -> p w e s", s=2),
+                in0=sine[v][:].rearrange("p (e w s) -> p w e s", e=2, s=2),
+                in1=coef_ps[:, g, :, f]
+                .rearrange("p (e s) -> p e s", s=2)
+                .unsqueeze(1)
+                .to_broadcast([P, SWEEP, 2, 2]),
                 op=ALU.mult,
             )
 
-        def quantise_basis(u):
-            s_codes[u] = three.tile([P, TOKENS], U32, align_bytes=64, name="s_codes", tag="s_codes")
-            s_scales[u] = three.tile([P, TOKENS], U8, align_bytes=64, name="s_scales", tag="s_scales")
+        def quantise_basis(v):
+            s_codes[v] = four.tile([P, SWEEP], U32, align_bytes=64, name="s_codes", tag="s_codes")
+            s_scales[v] = four.tile([P, SWEEP], U8, align_bytes=64, name="s_scales", tag="s_scales")
             nc.vector.quantize_mx(
-                out=s_codes[u][:].bitcast(FP8X4),
-                scales=s_scales[u][:],
-                in_=s_bf[u][:].rearrange("p w t -> p (w t)"),
+                out=s_codes[v][:].bitcast(FP8X4),
+                scales=s_scales[v][:],
+                in_=s_bf[v][:].rearrange("p w t -> p (w t)"),
             )
 
         def quantise_weights(u):
-            w_codes[u] = three.tile([P, O_TILES, P], U32, align_bytes=64, name="w_codes", tag="w_codes")
-            w_scales[u] = three.tile([P, O_TILES, P], U8, align_bytes=64, name="w_scales", tag="w_scales")
-            for lo, hi in ((0, 4), (4, 6)):
+            for lo, hi in CHUNKS:
                 nc.vector.quantize_mx(
-                    out=w_codes[u][:, lo:hi, :].rearrange("p j o -> p (j o)").bitcast(FP8X4),
-                    scales=w_scales[u][:, lo:hi, :].rearrange("p j o -> p (j o)"),
-                    in_=w_bf[u][:, lo:hi, :, :].rearrange("p j o t -> p (j o t)"),
+                    out=w_codes[:, u, lo:hi].bitcast(FP8X4),
+                    scales=w_scales[:, u, lo:hi],
+                    in_=w_bf[u][:, lo:hi, :].rearrange("p o t -> p (o t)"),
                 )
 
-        def multiply(u, j):
-            nc.tensor.matmul_mx(
-                out=acc[j][:],
-                lhsT=w_codes[u][:, j, :].bitcast(FP8X4),
-                lhsT_scale=w_scales[u][:, j, :],
-                rhs=s_codes[u][:].bitcast(FP8X4),
-                rhs_scale=s_scales[u][:],
-                start=(u == 0),
-                stop=(u == UNITS - 1),
+        def multiply(v):
+            h, u, g, f = where(v)
+            for i in range(S_TILES):
+                rows_i = slice(P * i, P * (i + 1))
+                for c, (lo, hi) in enumerate(CHUNKS):
+                    nc.tensor.matmul_mx(
+                        out=acc[h, i, c][:, 0 : hi - lo],
+                        lhsT=s_codes[v][:, rows_i].bitcast(FP8X4),
+                        lhsT_scale=s_scales[v][:, rows_i],
+                        rhs=w_codes[:, u, lo:hi].bitcast(FP8X4),
+                        rhs_scale=w_scales[:, u, lo:hi],
+                        start=(u == 0),
+                        stop=(u == UNITS - 1),
+                    )
+
+        def weight_pair(u, jj):
+            w_ps = psum_work.tile([P, 2, 2, P], F32, tag="work", name="w_ps")
+            for a in range(2):
+                for e in range(2):
+                    nc.tensor.transpose(
+                        w_ps[:, a, e, :],
+                        w_raw[u][:, 2 * jj + a, :].bitcast(F32)[:, e::2],
+                        ident_f32[:],
+                    )
+            nc.scalar.copy(
+                out=w_bf[u][:, 2 * P * jj : 2 * P * (jj + 1), :].rearrange("p (a o) t -> p a o t", a=2).bitcast(F32),
+                in_=w_ps[:].rearrange("p a e o -> p a o e"),
             )
 
-        def tensor_and_scalar_round(new, old):
-            if new is not None:
-                f, g = divmod(new, PASSES)
-                w_bf[new] = three.tile([P, O_TILES, P, PACK], BF16, align_bytes=64, name="w_bf", tag="w_bf")
-                sine[new] = three.tile([P, UNIT], F32, name="sine", tag="sine")
-            for jj in range(PAIRS):
-                if new is not None:
-                    wt_ps = psum_tp.tile([P, 2, 2, P], F32, tag="tp", name="wt_ps")
-                    for a in range(2):
-                        for e in range(2):
-                            nc.tensor.transpose(
-                                wt_ps[:, a, e, :],
-                                w_raw[f][:, 2 * jj + a, :].bitcast(F32)[:, WORDS * g + e : WORDS * (g + 1) : 2],
-                                ident_f32[:],
-                            )
-                    nc.scalar.copy(
-                        out=w_bf[new][:, 2 * jj : 2 * jj + 2, :, :].bitcast(F32),
-                        in_=wt_ps[:].rearrange("p a e o -> p a o e"),
+        def new_weights(u):
+            w_bf[u] = three.tile([P, OUT_DIM, PACK], BF16, align_bytes=64, name="w_bf", tag="w_bf")
+
+        def stage_x(h, g):
+            bank = psum_work.tile([P, 2, SWEEP], F32, tag="work", name="x_bank")
+            transpose_x(h, g, bank)
+            x_to_sbuf(h, g, bank)
+
+        def take_silu(h, g):
+            silu[h, g] = two.tile([P, SWEEP, PACK], BF16, align_bytes=64, name="silu", tag="silu")
+            nc.scalar.activation(
+                out=silu[h, g][:].rearrange("p w (e s) -> p w e s", s=2),
+                in_=x_t[h, g][:].rearrange("p e w -> p (e w)").bitcast(BF16).rearrange("p (e w s) -> p w e s", e=2, s=2),
+                func=ACT.Silu,
+            )
+
+        def quantise_silu(h, g):
+            silu_codes[h, g] = const.tile([P, SWEEP], U32, align_bytes=64, name="silu_codes_%d%d" % (h, g))
+            silu_scales[h, g] = const.tile([P, SWEEP], U8, align_bytes=64, name="silu_scales_%d%d" % (h, g))
+            nc.vector.quantize_mx(
+                out=silu_codes[h, g][:].bitcast(FP8X4),
+                scales=silu_scales[h, g][:],
+                in_=silu[h, g][:].rearrange("p w t -> p (w t)"),
+            )
+
+        def base_product(h, i, c):
+            lo, hi = CHUNKS[c]
+            rows_i = slice(P * i, P * (i + 1))
+            bank = psum_work.tile([P, BANK], F32, tag="work", name="base_ps")
+            for g in range(PASSES):
+                nc.tensor.matmul_mx(
+                    out=bank[:, 0 : hi - lo],
+                    lhsT=silu_codes[h, g][:, rows_i].bitcast(FP8X4),
+                    lhsT_scale=silu_scales[h, g][:, rows_i],
+                    rhs=base_codes[:, g, lo:hi].bitcast(FP8X4),
+                    rhs_scale=base_scales[:, g, lo:hi],
+                    start=(g == 0),
+                    stop=(g == PASSES - 1),
+                )
+            cols = base_sb[:, S_TILES * h + i, lo:hi]
+            nc.scalar.copy(out=cols, in_=bank[:, 0 : hi - lo])
+
+        def add_bias(h, i, c):
+            lo, hi = CHUNKS[c]
+            cols = base_sb[:, S_TILES * h + i, lo:hi]
+            nc.gpsimd.tensor_tensor(out=cols, in0=cols, in1=bias_bc[:, lo:hi], op=ALU.add)
+
+        def spread_row(r, c):
+            lo, hi = CHUNKS[c]
+            bank = psum_work.tile([P, BANK], F32, tag="work", name="row_ps")
+            nc.tensor.matmul(
+                out=bank[:, 0 : hi - lo], lhsT=ones_bf[:], rhs=rows[:, r, lo:hi], start=True, stop=True
+            )
+            return bank
+
+        def spread_gain(c):
+            lo, hi = CHUNKS[c]
+            nc.scalar.copy(out=gain_bc[:, lo:hi], in_=spread_row(1, c)[:, 0 : hi - lo])
+
+        def spread_bias(c):
+            lo, hi = CHUNKS[c]
+            cols = bias_bc[:, lo:hi]
+            nc.scalar.copy(out=cols, in_=spread_row(0, c)[:, 0 : hi - lo])
+            nc.gpsimd.tensor_tensor(out=cols, in0=cols, in1=gain_bc[:, lo:hi], op=ALU.mult)
+
+        def finish(h, i):
+            scaled = two.tile([P, OUT_DIM], F32, name="scaled", tag="scaled")
+            out_sb = two.tile([P, OUT_DIM], F32, name="out_sb", tag="out_sb")
+            for c, (lo, hi) in enumerate(CHUNKS):
+                nc.vector.tensor_mul(
+                    out=scaled[:, lo:hi], in0=acc[h, i, c][:, 0 : hi - lo], in1=gain_bc[:, lo:hi]
+                )
+            if h < SWEEPS - 1:
+                for lo in range(0, OUT_DIM, 2 * P):
+                    cols = slice(lo, lo + 2 * P)
+                    nc.gpsimd.tensor_tensor(
+                        out=out_sb[:, cols], in0=scaled[:, cols], in1=base_sb[:, S_TILES * h + i, cols], op=ALU.add
                     )
-                    if jj < 2:
-                        half = slice(UNIT // 2 * jj, UNIT // 2 * (jj + 1))
-                        nc.scalar.activation(
-                            out=sine[new][:, half], in_=frac[new][:, half], func=ACT.Sin, scale=2.0 * math.pi
-                        )
-                if old is not None:
-                    multiply(old, 2 * jj)
-                    multiply(old, 2 * jj + 1)
-            if new is not None and g == PASSES - 1 and f + W_BUFS < NUM_F:
-                load_weights(f + W_BUFS)
+            else:
+                nc.vector.tensor_add(out=out_sb[:], in0=scaled[:], in1=base_sb[:, S_TILES * h + i, :])
+            row = P * (S_TILES * h + i)
+            nc.sync.dma_start(out=outf[row : row + P, :], in_=out_sb[:])
+
+        def new_accumulators(h):
+            for i in range(S_TILES):
+                for c in range(len(CHUNKS)):
+                    acc[h, i, c] = psum.tile([P, BANK], F32, tag="acc%d%d" % (i, c), name="acc")
 
         nc.vector.tensor_scalar(
             out=turns[:], in0=grid_bc[:], scalar1=1.0 / (2.0 * math.pi), scalar2=None, op0=ALU.mult
         )
-        for g in range(PASSES):
-            for h in range(2):
-                xt_ps = psum_acc.tile([P, 2, HALF], F32, tag="acc%d" % (2 * g + h), name="xt_ps")
-                for e in range(2):
-                    for i in range(2):
-                        nc.tensor.transpose(
-                            xt_ps[:, e, P * i : P * (i + 1)],
-                            x_sb[:, 2 * h + i, :].bitcast(F32)[:, WORDS * g + e : WORDS * (g + 1) : 2],
-                            ident_f32[:],
-                        )
-                nc.vector.tensor_copy(
-                    out=x_t[:, g, HALF * h : HALF * (h + 1), :].bitcast(F32),
-                    in_=xt_ps[:].rearrange("p e w -> p w e"),
-                )
-            whole_turns(nc.vector, g)
-        for u in range(ANGLES_AHEAD):
-            reduce_angle(u)
-            if u + PASSES < ANGLES_AHEAD:
-                whole_turns(nc.vector, u + PASSES)
-        for u in range(ANGLES_AHEAD, ANGLES_AHEAD + 2):
-            whole_turns(nc.gpsimd, u)
-
-        silu = const.tile([P, PASSES, UNIT], BF16, align_bytes=64)
-        silu_codes = const.tile([P, PASSES, TOKENS], U32, align_bytes=64)
-        silu_scales = const.tile([P, PASSES, TOKENS], U8, align_bytes=64)
-        for g in range(PASSES):
-            nc.scalar.activation(
-                out=silu[:, g, :], in_=x_t[:, g, :, :].rearrange("p w t -> p (w t)"), func=ACT.Silu
-            )
-        rows_ps = psum_acc.tile([P, P], BF16, tag="acc4")
-        nc.tensor.transpose(rows_ps[:], rows[:], ident_bf[:])
+        x_to_psum(0, 0)
+        x_to_sbuf(0, 0, x_ps[0, 0])
         nc.tensor.matmul(
             out=coef_ps[:].rearrange("p g t f -> p (g t f)"),
             lhsT=ident_bf[:],
@@ -247,70 +387,84 @@ def tile_efficient_skan_batch_kernel(
             start=True,
             stop=True,
         )
-        for u in range(AHEAD):
-            tensor_and_scalar_round(u, None)
+        whole_turns(nc.vector, 0)
+        for v in range(1, TURNS_AHEAD):
+            whole_turns(nc.gpsimd, v)
+            if v <= ANGLES_AHEAD:
+                reduce_angle(v - 1)
+        for u in range(SINES_AHEAD):
+            if u < WEIGHTS_AHEAD:
+                new_weights(u)
+                weight_pair(u, 0)
+                weight_pair(u, 1)
+            take_sine(u)
+            if u < WEIGHTS_AHEAD:
+                weight_pair(u, 2)
+                load_weights(u + 4)
+        new_accumulators(0)
 
-        cols = const.tile([P, P], F32)
-        nc.vector.tensor_copy(out=cols[:], in_=rows_ps[:])
-        gain = cols[:, 64 : 64 + O_TILES]
-        bias = const.tile([P, O_TILES], F32)
-        nc.vector.tensor_reduce(
-            out=bias[:],
-            in_=cols[:, 0 : NUM_F * O_TILES].rearrange("p (f j) -> p j f", j=O_TILES),
-            axis=mybir.AxisListType.X,
-            op=ALU.add,
-        )
-        nc.vector.tensor_mul(out=bias[:], in0=bias[:], in1=gain)
-        for g in range(PASSES):
-            nc.vector.quantize_mx(
-                out=silu_codes[:, g, :].bitcast(FP8X4), scales=silu_scales[:, g, :], in_=silu[:, g, :]
-            )
+        extras = {}
 
-        base_sb = const.tile([P, O_TILES, TOKENS], F32)
-        for j in range(O_TILES):
-            o_cols = slice(P * j, P * (j + 1))
-            base_ps = psum_acc.tile([P, TOKENS], F32, tag="acc%d" % j, name="base_ps")
+        def at(step, call, *args):
+            extras.setdefault(step, []).append((call, args))
+
+        at(0, stage_x, 0, 1)
+        at(2, stage_x, 1, 0)
+        at(3, spread_gain, 0)
+        at(3, spread_gain, 1)
+        at(4, spread_bias, 0)
+        at(4, spread_bias, 1)
+        at(4, load_base)
+        at(5, stage_x, 1, 1)
+        for h in range(SWEEPS):
+            first = UNITS * h + 5
             for g in range(PASSES):
-                nc.tensor.matmul_mx(
-                    out=base_ps[:],
-                    lhsT=base_codes[:, g, o_cols].bitcast(FP8X4),
-                    lhsT_scale=base_scales[:, g, o_cols],
-                    rhs=silu_codes[:, g, :].bitcast(FP8X4),
-                    rhs_scale=silu_scales[:, g, :],
-                    start=(g == 0),
-                    stop=(g == PASSES - 1),
-                )
-            nc.scalar.activation(
-                out=base_sb[:, j, :], in_=base_ps[:], func=ACT.Identity, bias=bias[:, j : j + 1], scale=1.0
-            )
-        for j in range(O_TILES):
-            acc.append(psum_acc.tile([P, TOKENS], F32, tag="acc%d" % j, name="acc%d" % j))
+                at(first + g, take_silu, h, g)
+                at(first + 2 + g, quantise_silu, h, g)
+            for n in range(4):
+                at(first + 4 + n, base_product, h, n // 2, n % 2)
+                at(first + 5 + n, add_bias, h, n // 2, n % 2)
 
-        for u in range(UNITS):
-            quantise_weights(u)
-            basis(u)
-            if u + ANGLES_AHEAD < UNITS:
-                reduce_angle(u + ANGLES_AHEAD)
-            quantise_basis(u)
-            if u + ANGLES_AHEAD + 2 < UNITS:
-                whole_turns(nc.gpsimd, u + ANGLES_AHEAD + 2)
-            tensor_and_scalar_round(u + AHEAD if u + AHEAD < UNITS else None, u - 1 if u > 0 else None)
-        tensor_and_scalar_round(None, UNITS - 1)
-
-        out_view = outf.rearrange("(i p) o -> p i o", p=P)
-        for j in range(O_TILES):
-            out_t = two.tile([P, TOKENS], F32, name="out_t", tag="out_t")
-            nc.vector.scalar_tensor_tensor(
-                out=out_t[:],
-                in0=acc[j][:],
-                scalar=gain[:, j : j + 1],
-                in1=base_sb[:, j, :],
-                op0=ALU.mult,
-                op1=ALU.add,
-            )
-            back_ps = psum_acc.tile([P, TOK_TILES, P], F32, tag="acc%d" % j, name="back_ps")
-            for i in range(TOK_TILES):
-                nc.tensor.transpose(back_ps[:, i, :], out_t[:, P * i : P * (i + 1)], ident_f32[:])
-            out_sb = two.tile([P, TOK_TILES, P], F32, name="out_sb", tag="out_sb")
-            nc.scalar.copy(out=out_sb[:], in_=back_ps[:])
-            nc.sync.dma_start(out=out_view[:, :, P * j : P * (j + 1)], in_=out_sb[:])
+        for v in range(STEPS):
+            h, u, g, f = where(v)
+            if not by_tensor(v):
+                basis(v)
+            ahead = v + ANGLES_AHEAD
+            if ahead < STEPS:
+                reduce_angle(ahead)
+            if (ahead + 1) % NUM_F == 0 and ahead + 1 < STEPS:
+                x_to_psum(*where(ahead + 1)[0::2])
+            if h == 0:
+                quantise_weights(u)
+            quantise_basis(v)
+            if v + TURNS_AHEAD < STEPS:
+                whole_turns(nc.gpsimd, v + TURNS_AHEAD)
+            if v + 4 < STEPS and by_tensor(v + 4):
+                make_diagonals(v + 4)
+            new = v + WEIGHTS_AHEAD
+            if new < UNITS:
+                new_weights(new)
+                weight_pair(new, 0)
+                weight_pair(new, 1)
+            by = v + TENSOR_AHEAD
+            if by < STEPS and by_tensor(by):
+                basis_by_tensor(by, 0)
+            if v + SINES_AHEAD < STEPS:
+                take_sine(v + SINES_AHEAD)
+            if by < STEPS and by_tensor(by):
+                basis_by_tensor(by, 1)
+            if v > 0:
+                multiply(v - 1)
+                if v == UNITS:
+                    for i in range(S_TILES):
+                        finish(0, i)
+                    new_accumulators(1)
+            if new < UNITS:
+                weight_pair(new, 2)
+                if v + 6 < UNITS:
+                    load_weights(v + 6)
+            for call, args in extras.get(v, []):
+                call(*args)
+        multiply(STEPS - 1)
+        for i in range(S_TILES):
+            finish(1, i)

@@ -35,6 +35,7 @@ SINES_AHEAD = 3
 ANGLES_AHEAD = 5
 TURNS_AHEAD = 7
 CHUNKS = ((0, 512), (512, 768))
+PIECE = 256
 BANK = 512
 
 FLOPS = 2 * TOKENS * IN_DIM * OUT_DIM * (NUM_F + 1)
@@ -123,6 +124,7 @@ def tile_efficient_skan_batch_kernel(
         base_sb = const.tile([P, SWEEPS * S_TILES, OUT_DIM], F32)
         gain_bc = const.tile([P, OUT_DIM], F32)
         bias_bc = const.tile([P, OUT_DIM], F32)
+        coef_f32 = const.tile([P, PASSES, PACK, NUM_F], F32)
         x_ps = {}
         x_t = {}
         whole = {}
@@ -137,6 +139,8 @@ def tile_efficient_skan_batch_kernel(
         silu_codes = {}
         silu_scales = {}
         acc = {}
+        scaled = {}
+        out_sb = {}
 
         def where(v):
             h, u = divmod(v, UNITS)
@@ -162,7 +166,7 @@ def tile_efficient_skan_batch_kernel(
 
         def whole_turns(engine, v):
             h, u, g, f = where(v)
-            whole[v] = four.tile([P, STEP], I32, name="whole", tag="whole")
+            whole[v] = five.tile([P, STEP], I32, align_bytes=64, name="whole", tag="gate")
             engine.tensor_scalar(
                 out=whole[v][:],
                 in0=x_t[h, g][:].rearrange("p e w -> p (e w)").bitcast(BF16),
@@ -203,18 +207,11 @@ def tile_efficient_skan_batch_kernel(
             h, u, g, f = where(v)
             diag[v] = two.tile([P, PACK, P], F32, name="diag", tag="diag")
             for t in range(PACK):
-                nc.gpsimd.tensor_scalar(
-                    out=diag[v][:, t, :],
-                    in0=ident_f32[:],
-                    scalar1=coef_sb[:, g, t, f : f + 1],
-                    scalar2=0.0,
-                    op0=ALU.mult,
-                    op1=ALU.add,
+                nc.scalar.activation(
+                    out=diag[v][:, t, :], in_=ident_f32[:], func=ACT.Copy, scale=coef_f32[:, g, t, f : f + 1]
                 )
 
         def basis_by_tensor(v, i):
-            if i == 0:
-                s_bf[v] = four.tile([P, SWEEP, PACK], BF16, align_bytes=64, name="s_bf", tag="s_bf")
             bank = psum_work.tile([P, PACK, P], F32, tag="work", name="s_ps")
             for t in range(PACK):
                 nc.tensor.matmul(
@@ -228,9 +225,11 @@ def tile_efficient_skan_batch_kernel(
                 out=s_bf[v][:, P * i : P * (i + 1), :], in_=bank[:].rearrange("p t w -> p w t")
             )
 
+        def new_basis(v):
+            s_bf[v] = five.tile([P, SWEEP, PACK], BF16, align_bytes=64, name="s_bf", tag="gate")
+
         def basis(v):
             h, u, g, f = where(v)
-            s_bf[v] = four.tile([P, SWEEP, PACK], BF16, align_bytes=64, name="s_bf", tag="s_bf")
             nc.vector.tensor_tensor(
                 out=s_bf[v][:].rearrange("p w (e s) -> p w e s", s=2),
                 in0=sine[v][:].rearrange("p (e w s) -> p w e s", e=2, s=2),
@@ -329,10 +328,9 @@ def tile_efficient_skan_batch_kernel(
             cols = base_sb[:, S_TILES * h + i, lo:hi]
             nc.scalar.copy(out=cols, in_=bank[:, 0 : hi - lo])
 
-        def add_bias(h, i, c):
-            lo, hi = CHUNKS[c]
-            cols = base_sb[:, S_TILES * h + i, lo:hi]
-            nc.gpsimd.tensor_tensor(out=cols, in0=cols, in1=bias_bc[:, lo:hi], op=ALU.add)
+        def add_bias(h, i, n):
+            cols = base_sb[:, S_TILES * h + i, PIECE * n : PIECE * (n + 1)]
+            nc.gpsimd.tensor_tensor(out=cols, in0=cols, in1=bias_bc[:, PIECE * n : PIECE * (n + 1)], op=ALU.add)
 
         def spread_row(r, c):
             lo, hi = CHUNKS[c]
@@ -348,27 +346,30 @@ def tile_efficient_skan_batch_kernel(
 
         def spread_bias(c):
             lo, hi = CHUNKS[c]
-            cols = bias_bc[:, lo:hi]
-            nc.scalar.copy(out=cols, in_=spread_row(0, c)[:, 0 : hi - lo])
-            nc.gpsimd.tensor_tensor(out=cols, in0=cols, in1=gain_bc[:, lo:hi], op=ALU.mult)
+            nc.scalar.copy(out=bias_bc[:, lo:hi], in_=spread_row(0, c)[:, 0 : hi - lo])
 
-        def finish(h, i):
-            scaled = two.tile([P, OUT_DIM], F32, name="scaled", tag="scaled")
-            out_sb = two.tile([P, OUT_DIM], F32, name="out_sb", tag="out_sb")
+        def scale_bias(n):
+            cols = bias_bc[:, PIECE * n : PIECE * (n + 1)]
+            nc.gpsimd.tensor_tensor(out=cols, in0=cols, in1=gain_bc[:, PIECE * n : PIECE * (n + 1)], op=ALU.mult)
+
+        def scale_sums(h, i):
+            scaled[h, i] = two.tile([P, OUT_DIM], F32, name="scaled", tag="scaled")
+            out_sb[h, i] = two.tile([P, OUT_DIM], F32, name="out_sb", tag="out_sb")
             for c, (lo, hi) in enumerate(CHUNKS):
                 nc.vector.tensor_mul(
-                    out=scaled[:, lo:hi], in0=acc[h, i, c][:, 0 : hi - lo], in1=gain_bc[:, lo:hi]
+                    out=scaled[h, i][:, lo:hi], in0=acc[h, i, c][:, 0 : hi - lo], in1=gain_bc[:, lo:hi]
                 )
-            if h < SWEEPS - 1:
-                for lo in range(0, OUT_DIM, 2 * P):
-                    cols = slice(lo, lo + 2 * P)
-                    nc.gpsimd.tensor_tensor(
-                        out=out_sb[:, cols], in0=scaled[:, cols], in1=base_sb[:, S_TILES * h + i, cols], op=ALU.add
-                    )
-            else:
-                nc.vector.tensor_add(out=out_sb[:], in0=scaled[:], in1=base_sb[:, S_TILES * h + i, :])
-            row = P * (S_TILES * h + i)
-            nc.sync.dma_start(out=outf[row : row + P, :], in_=out_sb[:])
+
+        def add_base(engine, h, i, lo, hi):
+            engine.tensor_tensor(
+                out=out_sb[h, i][:, lo:hi],
+                in0=scaled[h, i][:, lo:hi],
+                in1=base_sb[:, S_TILES * h + i, lo:hi],
+                op=ALU.add,
+            )
+            if hi == OUT_DIM:
+                row = P * (S_TILES * h + i)
+                nc.sync.dma_start(out=outf[row : row + P, :], in_=out_sb[h, i][:])
 
         def new_accumulators(h):
             for i in range(S_TILES):
@@ -387,6 +388,7 @@ def tile_efficient_skan_batch_kernel(
             start=True,
             stop=True,
         )
+        nc.scalar.copy(out=coef_f32[:], in_=coef_ps[:])
         whole_turns(nc.vector, 0)
         for v in range(1, TURNS_AHEAD):
             whole_turns(nc.gpsimd, v)
@@ -402,6 +404,8 @@ def tile_efficient_skan_batch_kernel(
                 weight_pair(u, 2)
                 load_weights(u + 4)
         new_accumulators(0)
+        for v in range(TENSOR_AHEAD):
+            new_basis(v)
 
         extras = {}
 
@@ -416,14 +420,21 @@ def tile_efficient_skan_batch_kernel(
         at(4, spread_bias, 1)
         at(4, load_base)
         at(5, stage_x, 1, 1)
+        for n in range(OUT_DIM // PIECE):
+            at(6 + n, scale_bias, n)
         for h in range(SWEEPS):
-            first = UNITS * h + 5
+            first = UNITS * h + 3
             for g in range(PASSES):
                 at(first + g, take_silu, h, g)
                 at(first + 2 + g, quantise_silu, h, g)
-            for n in range(4):
-                at(first + 4 + n, base_product, h, n // 2, n % 2)
-                at(first + 5 + n, add_bias, h, n // 2, n % 2)
+            for i in range(S_TILES):
+                for c in range(len(CHUNKS)):
+                    at(first + 4 + 2 * i + c, base_product, h, i, c)
+                for n in range(OUT_DIM // PIECE):
+                    at(first + 7 + 3 * i + n, add_bias, h, i, n)
+        for i in range(S_TILES):
+            for n in range(OUT_DIM // PIECE):
+                at(UNITS + 1 + 3 * i + n, add_base, nc.gpsimd, 0, i, PIECE * n, PIECE * (n + 1))
 
         for v in range(STEPS):
             h, u, g, f = where(v)
@@ -437,10 +448,10 @@ def tile_efficient_skan_batch_kernel(
             if h == 0:
                 quantise_weights(u)
             quantise_basis(v)
+            if v + TENSOR_AHEAD < STEPS:
+                new_basis(v + TENSOR_AHEAD)
             if v + TURNS_AHEAD < STEPS:
                 whole_turns(nc.gpsimd, v + TURNS_AHEAD)
-            if v + 4 < STEPS and by_tensor(v + 4):
-                make_diagonals(v + 4)
             new = v + WEIGHTS_AHEAD
             if new < UNITS:
                 new_weights(new)
@@ -453,11 +464,13 @@ def tile_efficient_skan_batch_kernel(
                 take_sine(v + SINES_AHEAD)
             if by < STEPS and by_tensor(by):
                 basis_by_tensor(by, 1)
+            if by + 1 < STEPS and by_tensor(by + 1):
+                make_diagonals(by + 1)
             if v > 0:
                 multiply(v - 1)
                 if v == UNITS:
                     for i in range(S_TILES):
-                        finish(0, i)
+                        scale_sums(0, i)
                     new_accumulators(1)
             if new < UNITS:
                 weight_pair(new, 2)
@@ -467,4 +480,5 @@ def tile_efficient_skan_batch_kernel(
                 call(*args)
         multiply(STEPS - 1)
         for i in range(S_TILES):
-            finish(1, i)
+            scale_sums(1, i)
+            add_base(nc.vector, 1, i, 0, OUT_DIM)

@@ -118,6 +118,8 @@ def tile_efficient_skan_batch_kernel(
         nc.sync.dma_start(out=rows[0:1, 1, :], in_=scale_sp.rearrange("(a o) -> a o", a=1))
 
         turns = const.tile([P, NUM_F], F32)
+        period = const.tile([P, NUM_F], F32)
+        minus_grid = const.tile([P, NUM_F], F32)
         coef_ps = psum.tile([P, PASSES, PACK, NUM_F], F32, tag="coef")
         w_codes = const.tile([P, UNITS, OUT_DIM], U32, align_bytes=64)
         w_scales = const.tile([P, UNITS, OUT_DIM], U8, align_bytes=64)
@@ -181,24 +183,25 @@ def tile_efficient_skan_batch_kernel(
             frac[v] = five.tile([P, STEP], F32, name="frac", tag="frac")
             nc.vector.scalar_tensor_tensor(
                 out=frac[v][:],
-                in0=x_ps[h, g][:].rearrange("p e w -> p (e w)").bitcast(BF16),
-                scalar=turns[:, f : f + 1],
-                in1=whole[v][:],
+                in0=whole[v][:],
+                scalar=period[:, f : f + 1],
+                in1=x_ps[h, g][:].rearrange("p e w -> p (e w)").bitcast(BF16),
                 op0=ALU.mult,
                 op1=ALU.subtract,
             )
 
         def take_sine(v):
+            minus_g = minus_grid[:, v % NUM_F : v % NUM_F + 1]
             sine[v] = four.tile([P, STEP], F32, name="sine", tag="sine")
             if by_tensor(v):
                 nc.scalar.activation(
                     out=sine[v][:].rearrange("p (e s w) -> p e s w", e=2, s=2),
                     in_=frac[v][:].rearrange("p (e w s) -> p e s w", e=2, s=2),
                     func=ACT.Sin,
-                    scale=2.0 * math.pi,
+                    scale=minus_g,
                 )
             else:
-                nc.scalar.activation(out=sine[v][:], in_=frac[v][:], func=ACT.Sin, scale=2.0 * math.pi)
+                nc.scalar.activation(out=sine[v][:], in_=frac[v][:], func=ACT.Sin, scale=minus_g)
 
         def by_tensor(v):
             return v >= UNITS and v % 3 == 1
@@ -257,23 +260,36 @@ def tile_efficient_skan_batch_kernel(
                     in_=w_bf[u][:, lo:hi, :].rearrange("p o t -> p (o t)"),
                 )
 
-        def multiply(v):
+        def multiply(v, i):
             h, u, g, f = where(v)
-            for i in range(S_TILES):
-                rows_i = slice(P * i, P * (i + 1))
-                for c, (lo, hi) in enumerate(CHUNKS):
-                    nc.tensor.matmul_mx(
-                        out=acc[h, i, c][:, 0 : hi - lo],
-                        lhsT=s_codes[v][:, rows_i].bitcast(FP8X4),
-                        lhsT_scale=s_scales[v][:, rows_i],
-                        rhs=w_codes[:, u, lo:hi].bitcast(FP8X4),
-                        rhs_scale=w_scales[:, u, lo:hi],
-                        start=(u == 0),
-                        stop=(u == UNITS - 1),
-                    )
+            rows_i = slice(P * i, P * (i + 1))
+            for c, (lo, hi) in enumerate(CHUNKS):
+                nc.tensor.matmul_mx(
+                    out=acc[h, i, c][:, 0 : hi - lo],
+                    lhsT=s_codes[v][:, rows_i].bitcast(FP8X4),
+                    lhsT_scale=s_scales[v][:, rows_i],
+                    rhs=w_codes[:, u, lo:hi].bitcast(FP8X4),
+                    rhs_scale=w_scales[:, u, lo:hi],
+                    start=(u == 0),
+                    stop=(u == UNITS - 1),
+                )
+
+        def keep_warm(v, bank):
+            lo, hi = CHUNKS[0]
+            nc.tensor.matmul_mx(
+                out=bank,
+                lhsT=s_codes[v][:, 0:P].bitcast(FP8X4),
+                lhsT_scale=s_scales[v][:, 0:P],
+                rhs=w_codes[:, v, lo:hi].bitcast(FP8X4),
+                rhs_scale=w_scales[:, v, lo:hi],
+                start=True,
+                stop=True,
+            )
 
         def weight_pair(u, jj):
             w_ps = psum_work.tile([P, 2, 2, P], F32, tag="work", name="w_ps")
+            if jj == 0 and u >= 2 * WEIGHTS_AHEAD:
+                keep_warm(u - 2 * WEIGHTS_AHEAD, w_ps[:].rearrange("p a e o -> p (a e o)"))
             for a in range(2):
                 for e in range(2):
                     nc.tensor.transpose(
@@ -379,6 +395,15 @@ def tile_efficient_skan_batch_kernel(
         nc.vector.tensor_scalar(
             out=turns[:], in0=grid_bc[:], scalar1=1.0 / (2.0 * math.pi), scalar2=None, op0=ALU.mult
         )
+        nc.vector.tensor_scalar(out=period[:], in0=grid_bc[:], scalar1=0.0, scalar2=None, op0=ALU.is_equal)
+        nc.vector.tensor_scalar(
+            out=minus_grid[:], in0=grid_bc[:], scalar1=-1.0, scalar2=None, op0=ALU.mult
+        )
+        nc.vector.tensor_sub(out=period[:], in0=period[:], in1=minus_grid[:])
+        nc.vector.reciprocal(out=period[:], in_=period[:])
+        nc.vector.tensor_scalar(
+            out=period[:], in0=period[:], scalar1=2.0 * math.pi, scalar2=None, op0=ALU.mult
+        )
         x_to_psum(0, 0)
         x_to_sbuf(0, 0, x_ps[0, 0])
         nc.tensor.matmul(
@@ -457,6 +482,8 @@ def tile_efficient_skan_batch_kernel(
                 new_weights(new)
                 weight_pair(new, 0)
                 weight_pair(new, 1)
+            if v > 0:
+                multiply(v - 1, 0)
             by = v + TENSOR_AHEAD
             if by < STEPS and by_tensor(by):
                 basis_by_tensor(by, 0)
@@ -466,19 +493,20 @@ def tile_efficient_skan_batch_kernel(
                 basis_by_tensor(by, 1)
             if by + 1 < STEPS and by_tensor(by + 1):
                 make_diagonals(by + 1)
-            if v > 0:
-                multiply(v - 1)
-                if v == UNITS:
-                    for i in range(S_TILES):
-                        scale_sums(0, i)
-                    new_accumulators(1)
             if new < UNITS:
                 weight_pair(new, 2)
                 if v + 6 < UNITS:
                     load_weights(v + 6)
+            if v > 0:
+                multiply(v - 1, 1)
+                if v == UNITS:
+                    for i in range(S_TILES):
+                        scale_sums(0, i)
+                    new_accumulators(1)
             for call, args in extras.get(v, []):
                 call(*args)
-        multiply(STEPS - 1)
+        for i in range(S_TILES):
+            multiply(STEPS - 1, i)
         for i in range(S_TILES):
             scale_sums(1, i)
             add_base(nc.vector, 1, i, 0, OUT_DIM)

@@ -25,7 +25,6 @@ O_TILES = OUT_DIM // P
 SWEEPS = 2
 SWEEP = TOKENS // SWEEPS
 S_TILES = SWEEP // P
-WORDS = K_PASS // 2
 STEP = SWEEP * PACK
 UNITS = PASSES * NUM_F
 STEPS = SWEEPS * UNITS
@@ -59,14 +58,15 @@ def tile_efficient_skan_batch_kernel(
         psum_work = ctx.enter_context(tc.psum_pool(name="psum_work", bufs=2))
         ctx.enter_context(tc.manual_schedule())
 
-        x_sb = const.tile([P, SWEEPS * S_TILES, IN_DIM], BF16)
+        x_sb = {}
         x_view = xf.rearrange("(i p) k -> p i k", p=P)
         w_raw = {}
 
         def load_x(h, g):
             tiles = slice(S_TILES * h, S_TILES * (h + 1))
             k_cols = slice(K_PASS * g, K_PASS * (g + 1))
-            nc.sync.dma_start(out=x_sb[:, tiles, k_cols], in_=x_view[:, tiles, k_cols])
+            x_sb[h, g] = const.tile([P, S_TILES, K_PASS], BF16, name="x_sb_%d%d" % (h, g))
+            nc.sync.dma_start(out=x_sb[h, g][:], in_=x_view[:, tiles, k_cols])
 
         def load_weights(u):
             g, f = divmod(u, NUM_F)
@@ -154,7 +154,7 @@ def tile_efficient_skan_batch_kernel(
                 for i in range(S_TILES):
                     nc.tensor.transpose(
                         bank[:, e, P * i : P * (i + 1)],
-                        x_sb[:, S_TILES * h + i, :].bitcast(F32)[:, WORDS * g + e : WORDS * (g + 1) : 2],
+                        x_sb[h, g][:, i, :].bitcast(F32)[:, e::2],
                         ident_f32[:],
                     )
 
@@ -190,21 +190,22 @@ def tile_efficient_skan_batch_kernel(
                 op1=ALU.subtract,
             )
 
-        def take_sine(v):
-            minus_g = minus_grid[:, v % NUM_F : v % NUM_F + 1]
-            sine[v] = four.tile([P, STEP], F32, name="sine", tag="sine")
+        def take_sine(v, i):
+            if i == 0:
+                sine[v] = four.tile([P, STEP], F32, name="sine", tag="sine")
+            tokens = slice(P * i, P * (i + 1))
+            angles = frac[v][:].rearrange("p (e w s) -> p e w s", e=2, s=2)[:, :, tokens, :]
             if by_tensor(v):
-                nc.scalar.activation(
-                    out=sine[v][:].rearrange("p (e s w) -> p e s w", e=2, s=2),
-                    in_=frac[v][:].rearrange("p (e w s) -> p e s w", e=2, s=2),
-                    func=ACT.Sin,
-                    scale=minus_g,
-                )
+                sines = sine[v][:].rearrange("p (e s w) -> p e s w", e=2, s=2)[:, :, :, tokens]
+                angles = angles.rearrange("p e w s -> p e s w")
             else:
-                nc.scalar.activation(out=sine[v][:], in_=frac[v][:], func=ACT.Sin, scale=minus_g)
+                sines = sine[v][:].rearrange("p (w e s) -> p w e s", e=2, s=2)[:, tokens, :, :]
+                angles = angles.rearrange("p e w s -> p w e s")
+            f = v % NUM_F
+            nc.scalar.activation(out=sines, in_=angles, func=ACT.Sin, scale=minus_grid[:, f : f + 1])
 
         def by_tensor(v):
-            return v >= UNITS and v % 3 == 1
+            return v >= UNITS and v % 3 == 0
 
         def make_diagonals(v):
             h, u, g, f = where(v)
@@ -234,12 +235,9 @@ def tile_efficient_skan_batch_kernel(
         def basis(v):
             h, u, g, f = where(v)
             nc.vector.tensor_tensor(
-                out=s_bf[v][:].rearrange("p w (e s) -> p w e s", s=2),
-                in0=sine[v][:].rearrange("p (e w s) -> p w e s", e=2, s=2),
-                in1=coef_ps[:, g, :, f]
-                .rearrange("p (e s) -> p e s", s=2)
-                .unsqueeze(1)
-                .to_broadcast([P, SWEEP, 2, 2]),
+                out=s_bf[v][:],
+                in0=sine[v][:].rearrange("p (w t) -> p w t", t=PACK),
+                in1=coef_ps[:, g, :, f].unsqueeze(1).to_broadcast([P, SWEEP, PACK]),
                 op=ALU.mult,
             )
 
@@ -424,10 +422,11 @@ def tile_efficient_skan_batch_kernel(
                 new_weights(u)
                 weight_pair(u, 0)
                 weight_pair(u, 1)
-            take_sine(u)
+            take_sine(u, 0)
             if u < WEIGHTS_AHEAD:
                 weight_pair(u, 2)
                 load_weights(u + 4)
+            take_sine(u, 1)
         new_accumulators(0)
         for v in range(TENSOR_AHEAD):
             new_basis(v)
@@ -448,7 +447,7 @@ def tile_efficient_skan_batch_kernel(
         for n in range(OUT_DIM // PIECE):
             at(6 + n, scale_bias, n)
         for h in range(SWEEPS):
-            first = UNITS * h + 3
+            first = (8, 19)[h]
             for g in range(PASSES):
                 at(first + g, take_silu, h, g)
                 at(first + 2 + g, quantise_silu, h, g)
@@ -456,10 +455,10 @@ def tile_efficient_skan_batch_kernel(
                 for c in range(len(CHUNKS)):
                     at(first + 4 + 2 * i + c, base_product, h, i, c)
                 for n in range(OUT_DIM // PIECE):
-                    at(first + 7 + 3 * i + n, add_bias, h, i, n)
+                    at(first + 6 - h + 3 * i + n, add_bias, h, i, n)
         for i in range(S_TILES):
             for n in range(OUT_DIM // PIECE):
-                at(UNITS + 1 + 3 * i + n, add_base, nc.gpsimd, 0, i, PIECE * n, PIECE * (n + 1))
+                at(UNITS + 4 + 3 * i + n, add_base, nc.gpsimd, 0, i, PIECE * n, PIECE * (n + 1))
 
         for v in range(STEPS):
             h, u, g, f = where(v)
@@ -488,13 +487,16 @@ def tile_efficient_skan_batch_kernel(
             if by < STEPS and by_tensor(by):
                 basis_by_tensor(by, 0)
             if v + SINES_AHEAD < STEPS:
-                take_sine(v + SINES_AHEAD)
+                take_sine(v + SINES_AHEAD, 0)
             if by < STEPS and by_tensor(by):
                 basis_by_tensor(by, 1)
             if by + 1 < STEPS and by_tensor(by + 1):
                 make_diagonals(by + 1)
             if new < UNITS:
                 weight_pair(new, 2)
+            if v + SINES_AHEAD < STEPS:
+                take_sine(v + SINES_AHEAD, 1)
+            if new < UNITS:
                 if v + 6 < UNITS:
                     load_weights(v + 6)
             if v > 0:

@@ -81,8 +81,8 @@ def tile_efficient_skan_batch_kernel(
         nc.scalar.dma_start(out=grid_bc[:], in_=grid.partition_broadcast(P))
         coef_sb = const.tile([P, PASSES, PACK, NUM_F], BF16)
         nc.scalar.dma_start(
-            out=coef_sb[:].rearrange("p g t f -> p g (t f)"),
-            in_=coef.rearrange("(g p t) f -> p g (t f)", g=PASSES, t=PACK),
+            out=coef_sb[:].rearrange("p g (u s) f -> p (g u) (s f)", s=2),
+            in_=coef.rearrange("(a p s) f -> p a (s f)", p=P, s=2),
         )
         load_weights(0)
         load_x(0, 1)
@@ -113,11 +113,12 @@ def tile_efficient_skan_batch_kernel(
         nc.vector.memset(ones_bf[:], 1.0)
         nc.vector.memset(base_scales[:].bitcast(I32), 0)
         rows = const.tile([P, 2, OUT_DIM], BF16)
-        nc.gpsimd.memset(rows[:], 0.0)
+        nc.vector.memset(rows[:].bitcast(I32), 0)
         nc.sync.dma_start(out=rows[0:NUM_F, 0, :], in_=conv_b)
         nc.sync.dma_start(out=rows[0:1, 1, :], in_=scale_sp.rearrange("(a o) -> a o", a=1))
 
         turns = const.tile([P, NUM_F], F32)
+        turns_late = const.tile([P, NUM_F], F32)
         period = const.tile([P, NUM_F], F32)
         minus_grid = const.tile([P, NUM_F], F32)
         coef_ps = psum.tile([P, PASSES, PACK, NUM_F], F32, tag="coef")
@@ -144,23 +145,29 @@ def tile_efficient_skan_batch_kernel(
         scaled = {}
         out_sb = {}
 
+        def run_of_words(e):
+            return slice(P * e, P * (e + 1))
+
+        def every_second_word(e):
+            return slice(e, 2 * P, 2)
+
         def where(v):
             h, u = divmod(v, UNITS)
             g, f = divmod(u, NUM_F)
             return h, u, g, f
 
-        def transpose_x(h, g, bank):
+        def transpose_x(h, g, bank, words):
             for e in range(2):
                 for i in range(S_TILES):
                     nc.tensor.transpose(
                         bank[:, e, P * i : P * (i + 1)],
-                        x_sb[h, g][:, i, :].bitcast(F32)[:, e::2],
+                        x_sb[h, g][:, i, :].bitcast(F32)[:, words(e)],
                         ident_f32[:],
                     )
 
         def x_to_psum(h, g):
             x_ps[h, g] = psum.tile([P, 2, SWEEP], F32, tag="x", name="x_ps")
-            transpose_x(h, g, x_ps[h, g])
+            transpose_x(h, g, x_ps[h, g], run_of_words)
 
         def x_to_sbuf(h, g, bank):
             x_t[h, g] = const.tile([P, 2, SWEEP], F32, name="x_t_%d%d" % (h, g))
@@ -172,7 +179,7 @@ def tile_efficient_skan_batch_kernel(
             engine.tensor_scalar(
                 out=whole[v][:],
                 in0=x_t[h, g][:].rearrange("p e w -> p (e w)").bitcast(BF16),
-                scalar1=turns[:, f : f + 1],
+                scalar1=(turns if v == 0 else turns_late)[:, f : f + 1],
                 scalar2=0.0,
                 op0=ALU.mult,
                 op1=ALU.add,
@@ -205,7 +212,7 @@ def tile_efficient_skan_batch_kernel(
             nc.scalar.activation(out=sines, in_=angles, func=ACT.Sin, scale=minus_grid[:, f : f + 1])
 
         def by_tensor(v):
-            return v >= UNITS and v % 3 == 0
+            return v < 0
 
         def make_diagonals(v):
             h, u, g, f = where(v)
@@ -272,27 +279,13 @@ def tile_efficient_skan_batch_kernel(
                     stop=(u == UNITS - 1),
                 )
 
-        def keep_warm(v, bank):
-            lo, hi = CHUNKS[0]
-            nc.tensor.matmul_mx(
-                out=bank,
-                lhsT=s_codes[v][:, 0:P].bitcast(FP8X4),
-                lhsT_scale=s_scales[v][:, 0:P],
-                rhs=w_codes[:, v, lo:hi].bitcast(FP8X4),
-                rhs_scale=w_scales[:, v, lo:hi],
-                start=True,
-                stop=True,
-            )
-
         def weight_pair(u, jj):
             w_ps = psum_work.tile([P, 2, 2, P], F32, tag="work", name="w_ps")
-            if jj == 0 and u >= 2 * WEIGHTS_AHEAD:
-                keep_warm(u - 2 * WEIGHTS_AHEAD, w_ps[:].rearrange("p a e o -> p (a e o)"))
             for a in range(2):
                 for e in range(2):
                     nc.tensor.transpose(
                         w_ps[:, a, e, :],
-                        w_raw[u][:, 2 * jj + a, :].bitcast(F32)[:, e::2],
+                        w_raw[u][:, 2 * jj + a, :].bitcast(F32)[:, run_of_words(e)],
                         ident_f32[:],
                     )
             nc.scalar.copy(
@@ -305,14 +298,16 @@ def tile_efficient_skan_batch_kernel(
 
         def stage_x(h, g):
             bank = psum_work.tile([P, 2, SWEEP], F32, tag="work", name="x_bank")
-            transpose_x(h, g, bank)
+            transpose_x(h, g, bank, run_of_words)
             x_to_sbuf(h, g, bank)
 
         def take_silu(h, g):
+            bank = psum_work.tile([P, 2, SWEEP], F32, tag="work", name="silu_bank")
+            transpose_x(h, g, bank, every_second_word)
             silu[h, g] = two.tile([P, SWEEP, PACK], BF16, align_bytes=64, name="silu", tag="silu")
             nc.scalar.activation(
                 out=silu[h, g][:].rearrange("p w (e s) -> p w e s", s=2),
-                in_=x_t[h, g][:].rearrange("p e w -> p (e w)").bitcast(BF16).rearrange("p (e w s) -> p w e s", e=2, s=2),
+                in_=bank[:].rearrange("p e w -> p (e w)").bitcast(BF16).rearrange("p (e w s) -> p w e s", e=2, s=2),
                 func=ACT.Silu,
             )
 
@@ -413,6 +408,7 @@ def tile_efficient_skan_batch_kernel(
         )
         nc.scalar.copy(out=coef_f32[:], in_=coef_ps[:])
         whole_turns(nc.vector, 0)
+        nc.vector.tensor_copy(out=turns_late[:], in_=turns[:])
         for v in range(1, TURNS_AHEAD):
             whole_turns(nc.gpsimd, v)
             if v <= ANGLES_AHEAD:

@@ -29,12 +29,13 @@ STEP = SWEEP * PACK
 UNITS = PASSES * NUM_F
 STEPS = SWEEPS * UNITS
 WEIGHTS_AHEAD = 2
-TENSOR_AHEAD = 2
+BASIS_AHEAD = 2
 SINES_AHEAD = 3
 ANGLES_AHEAD = 5
 TURNS_AHEAD = 7
 CHUNKS = ((0, 512), (512, 768))
 PIECE = 256
+LAST_TILE = (SWEEPS - 1, S_TILES - 1)
 BANK = 512
 
 FLOPS = 2 * TOKENS * IN_DIM * OUT_DIM * (NUM_F + 1)
@@ -87,8 +88,6 @@ def tile_efficient_skan_batch_kernel(
         load_weights(0)
         load_x(0, 1)
         load_weights(1)
-        load_x(1, 0)
-        load_x(1, 1)
         load_weights(2)
         base_codes = const.tile([P, PASSES, OUT_DIM], U32, align_bytes=64)
         base_scales = const.tile([P, PASSES, OUT_DIM], U8, align_bytes=64)
@@ -111,6 +110,8 @@ def tile_efficient_skan_batch_kernel(
         make_identity(nc, ident_bf[:])
         ones_bf = const.tile([P, P], BF16)
         nc.vector.memset(ones_bf[:], 1.0)
+        first_silu = const.tile([P, 1], F32)
+        nc.scalar.activation(out=first_silu[:], in_=ones_bf[:, 0:1], func=ACT.Silu)
         nc.vector.memset(base_scales[:].bitcast(I32), 0)
         rows = const.tile([P, 2, OUT_DIM], BF16)
         nc.vector.memset(rows[:].bitcast(I32), 0)
@@ -127,14 +128,12 @@ def tile_efficient_skan_batch_kernel(
         base_sb = const.tile([P, SWEEPS * S_TILES, OUT_DIM], F32)
         gain_bc = const.tile([P, OUT_DIM], F32)
         bias_bc = const.tile([P, OUT_DIM], F32)
-        coef_f32 = const.tile([P, PASSES, PACK, NUM_F], F32)
         x_ps = {}
         x_t = {}
         whole = {}
         frac = {}
         sine = {}
         s_bf = {}
-        diag = {}
         s_codes = {}
         s_scales = {}
         w_bf = {}
@@ -143,7 +142,6 @@ def tile_efficient_skan_batch_kernel(
         silu_scales = {}
         acc = {}
         scaled = {}
-        out_sb = {}
 
         def run_of_words(e):
             return slice(P * e, P * (e + 1))
@@ -202,39 +200,10 @@ def tile_efficient_skan_batch_kernel(
                 sine[v] = four.tile([P, STEP], F32, name="sine", tag="sine")
             tokens = slice(P * i, P * (i + 1))
             angles = frac[v][:].rearrange("p (e w s) -> p e w s", e=2, s=2)[:, :, tokens, :]
-            if by_tensor(v):
-                sines = sine[v][:].rearrange("p (e s w) -> p e s w", e=2, s=2)[:, :, :, tokens]
-                angles = angles.rearrange("p e w s -> p e s w")
-            else:
-                sines = sine[v][:].rearrange("p (w e s) -> p w e s", e=2, s=2)[:, tokens, :, :]
-                angles = angles.rearrange("p e w s -> p w e s")
+            sines = sine[v][:].rearrange("p (w e s) -> p w e s", e=2, s=2)[:, tokens, :, :]
+            angles = angles.rearrange("p e w s -> p w e s")
             f = v % NUM_F
             nc.scalar.activation(out=sines, in_=angles, func=ACT.Sin, scale=minus_grid[:, f : f + 1])
-
-        def by_tensor(v):
-            return v < 0
-
-        def make_diagonals(v):
-            h, u, g, f = where(v)
-            diag[v] = two.tile([P, PACK, P], F32, name="diag", tag="diag")
-            for t in range(PACK):
-                nc.scalar.activation(
-                    out=diag[v][:, t, :], in_=ident_f32[:], func=ACT.Copy, scale=coef_f32[:, g, t, f : f + 1]
-                )
-
-        def basis_by_tensor(v, i):
-            bank = psum_work.tile([P, PACK, P], F32, tag="work", name="s_ps")
-            for t in range(PACK):
-                nc.tensor.matmul(
-                    out=bank[:, t, :],
-                    lhsT=diag[v][:, t, :],
-                    rhs=sine[v][:, SWEEP * t + P * i : SWEEP * t + P * (i + 1)],
-                    start=True,
-                    stop=True,
-                )
-            nc.scalar.copy(
-                out=s_bf[v][:, P * i : P * (i + 1), :], in_=bank[:].rearrange("p t w -> p w t")
-            )
 
         def new_basis(v):
             s_bf[v] = five.tile([P, SWEEP, PACK], BF16, align_bytes=64, name="s_bf", tag="gate")
@@ -279,8 +248,22 @@ def tile_efficient_skan_batch_kernel(
                     stop=(u == UNITS - 1),
                 )
 
+        def keep_warm(v, bank):
+            lo, hi = CHUNKS[0]
+            nc.tensor.matmul_mx(
+                out=bank,
+                lhsT=s_codes[v][:, 0:P].bitcast(FP8X4),
+                lhsT_scale=s_scales[v][:, 0:P],
+                rhs=w_codes[:, v, lo:hi].bitcast(FP8X4),
+                rhs_scale=w_scales[:, v, lo:hi],
+                start=True,
+                stop=True,
+            )
+
         def weight_pair(u, jj):
             w_ps = psum_work.tile([P, 2, 2, P], F32, tag="work", name="w_ps")
+            if jj == 0 and u >= 2 * WEIGHTS_AHEAD:
+                keep_warm(u - 2 * WEIGHTS_AHEAD, w_ps[:].rearrange("p a e o -> p (a e o)"))
             for a in range(2):
                 for e in range(2):
                     nc.tensor.transpose(
@@ -335,7 +318,10 @@ def tile_efficient_skan_batch_kernel(
                     stop=(g == PASSES - 1),
                 )
             cols = base_sb[:, S_TILES * h + i, lo:hi]
-            nc.scalar.copy(out=cols, in_=bank[:, 0 : hi - lo])
+            if (h, i) == LAST_TILE:
+                nc.vector.tensor_add(out=cols, in0=bank[:, 0 : hi - lo], in1=bias_bc[:, lo:hi])
+            else:
+                nc.scalar.copy(out=cols, in_=bank[:, 0 : hi - lo])
 
         def add_bias(h, i, n):
             cols = base_sb[:, S_TILES * h + i, PIECE * n : PIECE * (n + 1)]
@@ -363,22 +349,21 @@ def tile_efficient_skan_batch_kernel(
 
         def scale_sums(h, i):
             scaled[h, i] = two.tile([P, OUT_DIM], F32, name="scaled", tag="scaled")
-            out_sb[h, i] = two.tile([P, OUT_DIM], F32, name="out_sb", tag="out_sb")
             for c, (lo, hi) in enumerate(CHUNKS):
                 nc.vector.tensor_mul(
                     out=scaled[h, i][:, lo:hi], in0=acc[h, i, c][:, 0 : hi - lo], in1=gain_bc[:, lo:hi]
                 )
 
-        def add_base(engine, h, i, lo, hi):
+        def add_base(engine, h, i, lo, hi, pool, tag):
+            sums = pool.tile([P, hi - lo], F32, align_bytes=64, name="sums", tag=tag)
             engine.tensor_tensor(
-                out=out_sb[h, i][:, lo:hi],
+                out=sums[:],
                 in0=scaled[h, i][:, lo:hi],
                 in1=base_sb[:, S_TILES * h + i, lo:hi],
                 op=ALU.add,
             )
-            if hi == OUT_DIM:
-                row = P * (S_TILES * h + i)
-                nc.sync.dma_start(out=outf[row : row + P, :], in_=out_sb[h, i][:])
+            row = P * (S_TILES * h + i)
+            nc.sync.dma_start(out=outf[row : row + P, lo:hi], in_=sums[:])
 
         def new_accumulators(h):
             for i in range(S_TILES):
@@ -406,10 +391,11 @@ def tile_efficient_skan_batch_kernel(
             start=True,
             stop=True,
         )
-        nc.scalar.copy(out=coef_f32[:], in_=coef_ps[:])
         whole_turns(nc.vector, 0)
         nc.vector.tensor_copy(out=turns_late[:], in_=turns[:])
         for v in range(1, TURNS_AHEAD):
+            if v >= ANGLES_AHEAD:
+                new_basis(v - ANGLES_AHEAD)
             whole_turns(nc.gpsimd, v)
             if v <= ANGLES_AHEAD:
                 reduce_angle(v - 1)
@@ -424,8 +410,6 @@ def tile_efficient_skan_batch_kernel(
                 load_weights(u + 4)
             take_sine(u, 1)
         new_accumulators(0)
-        for v in range(TENSOR_AHEAD):
-            new_basis(v)
 
         extras = {}
 
@@ -433,33 +417,34 @@ def tile_efficient_skan_batch_kernel(
             extras.setdefault(step, []).append((call, args))
 
         at(0, stage_x, 0, 1)
-        at(2, stage_x, 1, 0)
-        at(3, spread_gain, 0)
-        at(3, spread_gain, 1)
-        at(4, spread_bias, 0)
-        at(4, spread_bias, 1)
-        at(4, load_base)
-        at(5, stage_x, 1, 1)
+        at(2, load_x, 1, 0)
+        at(4, load_x, 1, 1)
+        for c in range(len(CHUNKS)):
+            at(3, spread_gain, c)
+            at(4, spread_bias, c)
+        at(6, load_base)
+        at(7, stage_x, 1, 0)
+        at(15, stage_x, 1, 1)
         for n in range(OUT_DIM // PIECE):
-            at(6 + n, scale_bias, n)
-        for h in range(SWEEPS):
-            first = (8, 19)[h]
+            at(5 + n, scale_bias, n)
+        for h, first in enumerate((11, 18)):
             for g in range(PASSES):
                 at(first + g, take_silu, h, g)
                 at(first + 2 + g, quantise_silu, h, g)
             for i in range(S_TILES):
                 for c in range(len(CHUNKS)):
                     at(first + 4 + 2 * i + c, base_product, h, i, c)
-                for n in range(OUT_DIM // PIECE):
-                    at(first + 6 - h + 3 * i + n, add_bias, h, i, n)
-        for i in range(S_TILES):
-            for n in range(OUT_DIM // PIECE):
-                at(UNITS + 4 + 3 * i + n, add_base, nc.gpsimd, 0, i, PIECE * n, PIECE * (n + 1))
+        for n in range(6):
+            at(17 + n, add_bias, 0, n // 3, n % 3)
+        for n, step in enumerate((23, 24, 25, 26, 27, 28)):
+            pool, tag = (two, "early_sums") if step < 25 else (five, "gate")
+            at(step, add_base, nc.gpsimd, 0, n // 3, PIECE * (n % 3), PIECE * (n % 3 + 1), pool, tag)
+        for n, step in enumerate((25, 25, 26)):
+            at(step, add_bias, 1, 0, n)
 
         for v in range(STEPS):
             h, u, g, f = where(v)
-            if not by_tensor(v):
-                basis(v)
+            basis(v)
             ahead = v + ANGLES_AHEAD
             if ahead < STEPS:
                 reduce_angle(ahead)
@@ -468,8 +453,8 @@ def tile_efficient_skan_batch_kernel(
             if h == 0:
                 quantise_weights(u)
             quantise_basis(v)
-            if v + TENSOR_AHEAD < STEPS:
-                new_basis(v + TENSOR_AHEAD)
+            if v + BASIS_AHEAD < STEPS:
+                new_basis(v + BASIS_AHEAD)
             if v + TURNS_AHEAD < STEPS:
                 whole_turns(nc.gpsimd, v + TURNS_AHEAD)
             new = v + WEIGHTS_AHEAD
@@ -479,15 +464,8 @@ def tile_efficient_skan_batch_kernel(
                 weight_pair(new, 1)
             if v > 0:
                 multiply(v - 1, 0)
-            by = v + TENSOR_AHEAD
-            if by < STEPS and by_tensor(by):
-                basis_by_tensor(by, 0)
             if v + SINES_AHEAD < STEPS:
                 take_sine(v + SINES_AHEAD, 0)
-            if by < STEPS and by_tensor(by):
-                basis_by_tensor(by, 1)
-            if by + 1 < STEPS and by_tensor(by + 1):
-                make_diagonals(by + 1)
             if new < UNITS:
                 weight_pair(new, 2)
             if v + SINES_AHEAD < STEPS:
@@ -507,4 +485,4 @@ def tile_efficient_skan_batch_kernel(
             multiply(STEPS - 1, i)
         for i in range(S_TILES):
             scale_sums(1, i)
-            add_base(nc.vector, 1, i, 0, OUT_DIM)
+            add_base(nc.vector, 1, i, 0, OUT_DIM, two, "sums")

@@ -210,10 +210,21 @@ def tile_efficient_skan_batch_kernel(
 
         def basis(v):
             h, u, g, f = where(v)
+            mine = SWEEP - gpsimd_tokens(v)
             nc.vector.tensor_tensor(
-                out=s_bf[v][:],
-                in0=sine[v][:].rearrange("p (w t) -> p w t", t=PACK),
-                in1=coef_ps[:, g, :, f].unsqueeze(1).to_broadcast([P, SWEEP, PACK]),
+                out=s_bf[v][:, 0:mine, :],
+                in0=sine[v][:].rearrange("p (w t) -> p w t", t=PACK)[:, 0:mine, :],
+                in1=coef_ps[:, g, :, f].unsqueeze(1).to_broadcast([P, mine, PACK]),
+                op=ALU.mult,
+            )
+
+        def basis_by_gpsimd(v):
+            h, u, g, f = where(v)
+            n = gpsimd_tokens(v)
+            nc.gpsimd.tensor_tensor(
+                out=s_bf[v][:, SWEEP - n : SWEEP, :],
+                in0=sine[v][:].rearrange("p (w t) -> p w t", t=PACK)[:, SWEEP - n : SWEEP, :],
+                in1=coef_sb[:, g, :, f].unsqueeze(1).to_broadcast([P, n, PACK]),
                 op=ALU.mult,
             )
 
@@ -409,6 +420,8 @@ def tile_efficient_skan_batch_kernel(
                 weight_pair(u, 2)
                 load_weights(u + 4)
             take_sine(u, 1)
+        for g in range(PASSES):
+            take_silu(0, g)
         new_accumulators(0)
 
         extras = {}
@@ -417,20 +430,23 @@ def tile_efficient_skan_batch_kernel(
             extras.setdefault(step, []).append((call, args))
 
         at(0, stage_x, 0, 1)
+        for g in range(PASSES):
+            at(g, quantise_silu, 0, g)
         at(2, load_x, 1, 0)
         at(4, load_x, 1, 1)
         for c in range(len(CHUNKS)):
-            at(3, spread_gain, c)
-            at(4, spread_bias, c)
+            at(2 + c, spread_gain, c)
+            at(4 + c, spread_bias, c)
         at(6, load_base)
         at(7, stage_x, 1, 0)
         at(15, stage_x, 1, 1)
         for n in range(OUT_DIM // PIECE):
-            at(5 + n, scale_bias, n)
+            at(6 + n, scale_bias, n)
         for h, first in enumerate((11, 18)):
-            for g in range(PASSES):
-                at(first + g, take_silu, h, g)
-                at(first + 2 + g, quantise_silu, h, g)
+            if h > 0:
+                for g in range(PASSES):
+                    at(first + g, take_silu, h, g)
+                    at(first + 2 + g, quantise_silu, h, g)
             for i in range(S_TILES):
                 for c in range(len(CHUNKS)):
                     at(first + 4 + 2 * i + c, base_product, h, i, c)
@@ -441,6 +457,13 @@ def tile_efficient_skan_batch_kernel(
             at(step, add_base, nc.gpsimd, 0, n // 3, PIECE * (n % 3), PIECE * (n % 3 + 1), pool, tag)
         for n, step in enumerate((25, 25, 26)):
             at(step, add_bias, 1, 0, n)
+
+        gpsimd_calls = (scale_bias, add_bias, add_base)
+
+        def gpsimd_tokens(v):
+            if v < 2 or any([call in gpsimd_calls for call, args in extras.get(v - 1, [])]):
+                return 0
+            return (64 if v < UNITS else 32)
 
         for v in range(STEPS):
             h, u, g, f = where(v)
@@ -457,6 +480,8 @@ def tile_efficient_skan_batch_kernel(
                 new_basis(v + BASIS_AHEAD)
             if v + TURNS_AHEAD < STEPS:
                 whole_turns(nc.gpsimd, v + TURNS_AHEAD)
+            if v + 1 < STEPS and gpsimd_tokens(v + 1) > 0:
+                basis_by_gpsimd(v + 1)
             new = v + WEIGHTS_AHEAD
             if new < UNITS:
                 new_weights(new)

@@ -78,6 +78,8 @@ def tile_efficient_skan_batch_kernel(
             )
 
         load_x(0, 0)
+        rows = const.tile([P, 2, OUT_DIM], BF16)
+        nc.vector.memset(rows[:].bitcast(I32), 0)
         grid_bc = const.tile([P, NUM_F], BF16)
         nc.scalar.dma_start(out=grid_bc[:], in_=grid.partition_broadcast(P))
         coef_sb = const.tile([P, PASSES, PACK, NUM_F], BF16)
@@ -85,6 +87,8 @@ def tile_efficient_skan_batch_kernel(
             out=coef_sb[:].rearrange("p g (u s) f -> p (g u) (s f)", s=2),
             in_=coef.rearrange("(a p s) f -> p a (s f)", p=P, s=2),
         )
+        nc.sync.dma_start(out=rows[0:NUM_F, 0, :], in_=conv_b)
+        nc.sync.dma_start(out=rows[0:1, 1, :], in_=scale_sp.rearrange("(a o) -> a o", a=1))
         load_weights(0)
         load_x(0, 1)
         load_weights(1)
@@ -113,10 +117,6 @@ def tile_efficient_skan_batch_kernel(
         first_silu = const.tile([P, 1], F32)
         nc.scalar.activation(out=first_silu[:], in_=ones_bf[:, 0:1], func=ACT.Silu)
         nc.vector.memset(base_scales[:].bitcast(I32), 0)
-        rows = const.tile([P, 2, OUT_DIM], BF16)
-        nc.vector.memset(rows[:].bitcast(I32), 0)
-        nc.sync.dma_start(out=rows[0:NUM_F, 0, :], in_=conv_b)
-        nc.sync.dma_start(out=rows[0:1, 1, :], in_=scale_sp.rearrange("(a o) -> a o", a=1))
 
         turns = const.tile([P, NUM_F], F32)
         turns_late = const.tile([P, NUM_F], F32)
@@ -273,7 +273,7 @@ def tile_efficient_skan_batch_kernel(
 
         def weight_pair(u, jj):
             w_ps = psum_work.tile([P, 2, 2, P], F32, tag="work", name="w_ps")
-            if jj == 0 and u >= 2 * WEIGHTS_AHEAD:
+            if jj == 0 and u >= 2 * WEIGHTS_AHEAD and u % NUM_F not in (4, 5):
                 keep_warm(u - 2 * WEIGHTS_AHEAD, w_ps[:].rearrange("p a e o -> p (a e o)"))
             for a in range(2):
                 for e in range(2):
@@ -365,8 +365,8 @@ def tile_efficient_skan_batch_kernel(
                     out=scaled[h, i][:, lo:hi], in0=acc[h, i, c][:, 0 : hi - lo], in1=gain_bc[:, lo:hi]
                 )
 
-        def add_base(engine, h, i, lo, hi, pool, tag):
-            sums = pool.tile([P, hi - lo], F32, align_bytes=64, name="sums", tag=tag)
+        def add_base(engine, h, i, lo, hi):
+            sums = two.tile([P, hi - lo], F32, name="sums", tag="sums%d" % h)
             engine.tensor_tensor(
                 out=sums[:],
                 in0=scaled[h, i][:, lo:hi],
@@ -390,9 +390,6 @@ def tile_efficient_skan_batch_kernel(
         )
         nc.vector.tensor_sub(out=period[:], in0=period[:], in1=minus_grid[:])
         nc.vector.reciprocal(out=period[:], in_=period[:])
-        nc.vector.tensor_scalar(
-            out=period[:], in0=period[:], scalar1=2.0 * math.pi, scalar2=None, op0=ALU.mult
-        )
         x_to_psum(0, 0)
         x_to_sbuf(0, 0, x_ps[0, 0])
         nc.tensor.matmul(
@@ -403,7 +400,13 @@ def tile_efficient_skan_batch_kernel(
             stop=True,
         )
         whole_turns(nc.vector, 0)
+        nc.vector.tensor_scalar(
+            out=period[:], in0=period[:], scalar1=2.0 * math.pi, scalar2=None, op0=ALU.mult
+        )
         nc.vector.tensor_copy(out=turns_late[:], in_=turns[:])
+        for c in range(len(CHUNKS)):
+            spread_gain(c)
+            spread_bias(c)
         for v in range(1, TURNS_AHEAD):
             if v >= ANGLES_AHEAD:
                 new_basis(v - ANGLES_AHEAD)
@@ -420,8 +423,6 @@ def tile_efficient_skan_batch_kernel(
                 weight_pair(u, 2)
                 load_weights(u + 4)
             take_sine(u, 1)
-        for g in range(PASSES):
-            take_silu(0, g)
         new_accumulators(0)
 
         extras = {}
@@ -431,44 +432,39 @@ def tile_efficient_skan_batch_kernel(
 
         at(0, stage_x, 0, 1)
         for g in range(PASSES):
-            at(g, quantise_silu, 0, g)
-        at(2, load_x, 1, 0)
-        at(4, load_x, 1, 1)
-        for c in range(len(CHUNKS)):
-            at(2 + c, spread_gain, c)
-            at(4 + c, spread_bias, c)
-        at(6, load_base)
-        at(7, stage_x, 1, 0)
-        at(15, stage_x, 1, 1)
-        for n in range(OUT_DIM // PIECE):
+            at(13 + g, take_silu, 0, g)
+            at(15 + g, quantise_silu, 0, g)
+            at(2 + 2 * g, load_x, 1, g)
+            at(7 + 8 * g, stage_x, 1, g)
+            at(18 + g, take_silu, 1, g)
+            at(21 + g, quantise_silu, 1, g)
+        at(5, load_base)
+        for n in range(3):
             at(6 + n, scale_bias, n)
-        for h, first in enumerate((11, 18)):
-            if h > 0:
-                for g in range(PASSES):
-                    at(first + g, take_silu, h, g)
-                    at(first + 2 + g, quantise_silu, h, g)
-            for i in range(S_TILES):
-                for c in range(len(CHUNKS)):
-                    at(first + 4 + 2 * i + c, base_product, h, i, c)
-        for n in range(6):
-            at(17 + n, add_bias, 0, n // 3, n % 3)
-        for n, step in enumerate((23, 24, 25, 26, 27, 28)):
-            pool, tag = (two, "early_sums") if step < 25 else (five, "gate")
-            at(step, add_base, nc.gpsimd, 0, n // 3, PIECE * (n % 3), PIECE * (n % 3 + 1), pool, tag)
-        for n, step in enumerate((25, 25, 26)):
-            at(step, add_bias, 1, 0, n)
+        for i in range(S_TILES):
+            for c in range(len(CHUNKS)):
+                at(17 + i, base_product, 0, i, c)
+                at(23 + i, base_product, 1, i, c)
+            for n in range(3):
+                at(17 + 3 * i + n, add_bias, 0, i, n)
+                at((23, 24, 25, 25, 26, 26)[3 * i + n], add_base, nc.gpsimd, 0, i, PIECE * n, PIECE * (n + 1))
+        for n in range(3):
+            at(27 + n, add_bias, 1, 0, n)
 
         gpsimd_calls = (scale_bias, add_bias, add_base)
 
         def gpsimd_tokens(v):
             if v < 2 or any([call in gpsimd_calls for call, args in extras.get(v - 1, [])]):
                 return 0
-            return (64 if v < UNITS else 32)
+            return 32 if v < STEPS - 4 else 0
 
         for v in range(STEPS):
             h, u, g, f = where(v)
-            basis(v)
             ahead = v + ANGLES_AHEAD
+            if ahead <= STEPS:
+                basis(v)
+            if ahead >= STEPS and v + 1 < STEPS:
+                basis(v + 1)
             if ahead < STEPS:
                 reduce_angle(ahead)
             if (ahead + 1) % NUM_F == 0 and ahead + 1 < STEPS:
@@ -510,4 +506,5 @@ def tile_efficient_skan_batch_kernel(
             multiply(STEPS - 1, i)
         for i in range(S_TILES):
             scale_sums(1, i)
-            add_base(nc.vector, 1, i, 0, OUT_DIM, two, "sums")
+        for i in range(S_TILES):
+            add_base(nc.vector, 1, i, 0, OUT_DIM)

@@ -142,6 +142,7 @@ def tile_efficient_skan_batch_kernel(
         silu_scales = {}
         acc = {}
         scaled = {}
+        last_base = {}
 
         def run_of_words(e):
             return slice(P * e, P * (e + 1))
@@ -328,11 +329,16 @@ def tile_efficient_skan_batch_kernel(
                     start=(g == 0),
                     stop=(g == PASSES - 1),
                 )
-            cols = base_sb[:, S_TILES * h + i, lo:hi]
             if (h, i) == LAST_TILE:
-                nc.vector.tensor_add(out=cols, in0=bank[:, 0 : hi - lo], in1=bias_bc[:, lo:hi])
+                last_base[c] = bank
             else:
-                nc.scalar.copy(out=cols, in_=bank[:, 0 : hi - lo])
+                nc.scalar.copy(out=base_sb[:, S_TILES * h + i, lo:hi], in_=bank[:, 0 : hi - lo])
+
+        def last_bias(c):
+            lo, hi = CHUNKS[c]
+            nc.vector.tensor_add(
+                out=base_sb[:, SWEEPS * S_TILES - 1, lo:hi], in0=last_base[c][:, 0 : hi - lo], in1=bias_bc[:, lo:hi]
+            )
 
         def add_bias(h, i, n):
             cols = base_sb[:, S_TILES * h + i, PIECE * n : PIECE * (n + 1)]
@@ -445,6 +451,7 @@ def tile_efficient_skan_batch_kernel(
             for c in range(len(CHUNKS)):
                 at(17 + i, base_product, 0, i, c)
                 at(23 + i, base_product, 1, i, c)
+            at(STEPS - 1, last_bias, i)
             for n in range(3):
                 at(17 + 3 * i + n, add_bias, 0, i, n)
                 at((23, 24, 25, 25, 26, 26)[3 * i + n], add_base, nc.gpsimd, 0, i, PIECE * n, PIECE * (n + 1))

@@ -178,7 +178,7 @@ def tile_efficient_skan_batch_kernel(
             engine.tensor_scalar(
                 out=whole[v][:],
                 in0=x_t[h, g][:].rearrange("p e w -> p (e w)").bitcast(BF16),
-                scalar1=(turns if v == 0 else turns_late)[:, f : f + 1],
+                scalar1=(turns if v < 2 else turns_late)[:, f : f + 1],
                 scalar2=0.0,
                 op0=ALU.mult,
                 op1=ALU.add,
@@ -274,7 +274,7 @@ def tile_efficient_skan_batch_kernel(
 
         def weight_pair(u, jj):
             w_ps = psum_work.tile([P, 2, 2, P], F32, tag="work", name="w_ps")
-            if jj == 0 and u >= 2 * WEIGHTS_AHEAD and u % NUM_F not in (4, 5):
+            if jj == 0 and u >= 2 * WEIGHTS_AHEAD:
                 keep_warm(u - 2 * WEIGHTS_AHEAD, w_ps[:].rearrange("p a e o -> p (a e o)"))
             for a in range(2):
                 for e in range(2):
@@ -340,9 +340,9 @@ def tile_efficient_skan_batch_kernel(
                 out=base_sb[:, SWEEPS * S_TILES - 1, lo:hi], in0=last_base[c][:, 0 : hi - lo], in1=bias_bc[:, lo:hi]
             )
 
-        def add_bias(h, i, n):
-            cols = base_sb[:, S_TILES * h + i, PIECE * n : PIECE * (n + 1)]
-            nc.gpsimd.tensor_tensor(out=cols, in0=cols, in1=bias_bc[:, PIECE * n : PIECE * (n + 1)], op=ALU.add)
+        def add_bias(h, i, lo, hi):
+            cols = base_sb[:, S_TILES * h + i, lo:hi]
+            nc.gpsimd.tensor_tensor(out=cols, in0=cols, in1=bias_bc[:, lo:hi], op=ALU.add)
 
         def spread_row(r, c):
             lo, hi = CHUNKS[c]
@@ -371,8 +371,8 @@ def tile_efficient_skan_batch_kernel(
                     out=scaled[h, i][:, lo:hi], in0=acc[h, i, c][:, 0 : hi - lo], in1=gain_bc[:, lo:hi]
                 )
 
-        def add_base(engine, h, i, lo, hi):
-            sums = two.tile([P, hi - lo], F32, name="sums", tag="sums%d" % h)
+        def add_base(engine, h, i, lo, hi, pool, tag):
+            sums = pool.tile([P, hi - lo], F32, align_bytes=64, name="sums", tag=tag)
             engine.tensor_tensor(
                 out=sums[:],
                 in0=scaled[h, i][:, lo:hi],
@@ -405,7 +405,8 @@ def tile_efficient_skan_batch_kernel(
             start=True,
             stop=True,
         )
-        whole_turns(nc.vector, 0)
+        for v in range(2):
+            whole_turns(nc.vector, v)
         nc.vector.tensor_scalar(
             out=period[:], in0=period[:], scalar1=2.0 * math.pi, scalar2=None, op0=ALU.mult
         )
@@ -416,7 +417,8 @@ def tile_efficient_skan_batch_kernel(
         for v in range(1, TURNS_AHEAD):
             if v >= ANGLES_AHEAD:
                 new_basis(v - ANGLES_AHEAD)
-            whole_turns(nc.gpsimd, v)
+            if v > 1:
+                whole_turns(nc.gpsimd, v)
             if v <= ANGLES_AHEAD:
                 reduce_angle(v - 1)
         for u in range(SINES_AHEAD):
@@ -453,10 +455,14 @@ def tile_efficient_skan_batch_kernel(
                 at(23 + i, base_product, 1, i, c)
             at(STEPS - 1, last_bias, i)
             for n in range(3):
-                at(17 + 3 * i + n, add_bias, 0, i, n)
-                at((23, 24, 25, 25, 26, 26)[3 * i + n], add_base, nc.gpsimd, 0, i, PIECE * n, PIECE * (n + 1))
-        for n in range(3):
-            at(27 + n, add_bias, 1, 0, n)
+                at(17 + 3 * i + n, add_bias, 0, i, PIECE * n, PIECE * (n + 1))
+        at(23, add_base, nc.gpsimd, 0, 0, 0, 256, two, "sums_early")
+        at(24, add_base, nc.gpsimd, 0, 0, 256, 512, two, "sums_early")
+        at(25, add_base, nc.gpsimd, 0, 0, 512, 768, five, "gate")
+        at(25, add_base, nc.gpsimd, 0, 1, 0, 512, two, "sums_512")
+        at(26, add_base, nc.gpsimd, 0, 1, 512, 768, five, "gate")
+        at(26, add_bias, 1, 0, 0, 512)
+        at(27, add_bias, 1, 0, 512, 768)
 
         gpsimd_calls = (scale_bias, add_bias, add_base)
 
@@ -514,4 +520,5 @@ def tile_efficient_skan_batch_kernel(
         for i in range(S_TILES):
             scale_sums(1, i)
         for i in range(S_TILES):
-            add_base(nc.vector, 1, i, 0, OUT_DIM)
+            for c, (lo, hi) in enumerate(CHUNKS):
+                add_base(nc.vector, 1, i, lo, hi, two, "sums_last%d" % c)

import math
from contextlib import ExitStack

import concourse.mybir as mybir
from concourse.masks import make_identity

F32 = mybir.dt.float32
BF16 = mybir.dt.bfloat16
I32 = mybir.dt.int32
U32 = mybir.dt.uint32
U8 = mybir.dt.uint8
FP8X4 = mybir.dt.float8_e4m3fn_x4
ALU = mybir.AluOpType
ACT = mybir.ActivationFunctionType

P = 128
PACK = 4
K_PASS = P * PACK
TOKENS = 512
IN_DIM = 1024
OUT_DIM = 768
NUM_F = 8
PASSES = IN_DIM // K_PASS
O_TILES = OUT_DIM // P
SWEEPS = 2
SWEEP = TOKENS // SWEEPS
S_TILES = SWEEP // P
STEP = SWEEP * PACK
UNITS = PASSES * NUM_F
STEPS = SWEEPS * UNITS
WEIGHTS_AHEAD = 2
BASIS_AHEAD = 2
SINES_AHEAD = 3
ANGLES_AHEAD = 5
TURNS_AHEAD = 7
CHUNKS = ((0, 512), (512, 768))
PIECE = 256
LAST_TILE = (SWEEPS - 1, S_TILES - 1)
BANK = 512

FLOPS = 2 * TOKENS * IN_DIM * OUT_DIM * (NUM_F + 1)


def tile_efficient_skan_batch_kernel(
    tc, x, base_weight_words, base_weight_scales, grid, scale_sp, coef, conv_w, conv_b, out
):
    nc = tc.nc
    xf = x.flatten_outer_dims()
    outf = out.flatten_outer_dims()

    with ExitStack() as ctx:
        const = ctx.enter_context(tc.tile_pool(name="const", bufs=1))
        wpool = ctx.enter_context(tc.tile_pool(name="wpool", bufs=4))
        two = ctx.enter_context(tc.tile_pool(name="two", bufs=2))
        three = ctx.enter_context(tc.tile_pool(name="three", bufs=3))
        five = ctx.enter_context(tc.tile_pool(name="five", bufs=5))
        four = ctx.enter_context(tc.tile_pool(name="four", bufs=4))
        psum = ctx.enter_context(tc.psum_pool(name="psum", bufs=1))
        psum_work = ctx.enter_context(tc.psum_pool(name="psum_work", bufs=2))
        ctx.enter_context(tc.manual_schedule())

        x_sb = {}
        x_view = xf.rearrange("(i p) k -> p i k", p=P)
        w_raw = {}

        def load_x(h, g):
            tiles = slice(S_TILES * h, S_TILES * (h + 1))
            k_cols = slice(K_PASS * g, K_PASS * (g + 1))
            x_sb[h, g] = const.tile([P, S_TILES, K_PASS], BF16, name="x_sb_%d%d" % (h, g))
            nc.sync.dma_start(out=x_sb[h, g][:], in_=x_view[:, tiles, k_cols])

        def load_weights(u):
            g, f = divmod(u, NUM_F)
            w_raw[u] = wpool.tile([P, O_TILES, K_PASS], BF16, name="w_raw", tag="w_raw")
            nc.sync.dma_start(
                out=w_raw[u][:],
                in_=conv_w[f, :, K_PASS * g : K_PASS * (g + 1)].rearrange("(j p) k -> p j k", p=P),
            )

        load_x(0, 0)
        rows = const.tile([P, 2, OUT_DIM], BF16)
        nc.vector.memset(rows[:].bitcast(I32), 0)
        grid_bc = const.tile([P, NUM_F], BF16)
        nc.scalar.dma_start(out=grid_bc[:], in_=grid.partition_broadcast(P))
        coef_sb = const.tile([P, PASSES, PACK, NUM_F], BF16)
        nc.scalar.dma_start(
            out=coef_sb[:].rearrange("p g (u s) f -> p (g u) (s f)", s=2),
            in_=coef.rearrange("(a p s) f -> p a (s f)", p=P, s=2),
        )
        nc.sync.dma_start(out=rows[0:NUM_F, 0, :], in_=conv_b)
        nc.sync.dma_start(out=rows[0:1, 1, :], in_=scale_sp.rearrange("(a o) -> a o", a=1))
        load_weights(0)
        load_x(0, 1)
        load_weights(1)
        load_weights(2)
        base_codes = const.tile([P, PASSES, OUT_DIM], U32, align_bytes=64)
        base_scales = const.tile([P, PASSES, OUT_DIM], U8, align_bytes=64)
        load_weights(3)

        def load_base():
            nc.sync.dma_start(
                out=base_codes[:].bitcast(I32),
                in_=base_weight_words.rearrange("g p n t -> p g (n t)").bitcast(I32),
            )
            for q in range(4):
                nc.sync.dma_start(
                    out=base_scales[32 * q : 32 * q + 4, :, :].bitcast(I32),
                    in_=base_weight_scales[:, 4 * q : 4 * q + 4, :].rearrange("g r n -> r g n").bitcast(I32),
                )

        ident_f32 = const.tile([P, P], F32)
        make_identity(nc, ident_f32[:])
        ident_bf = const.tile([P, P], BF16)
        make_identity(nc, ident_bf[:])
        ones_bf = const.tile([P, P], BF16)
        nc.vector.memset(ones_bf[:], 1.0)
        first_silu = const.tile([P, 1], F32)
        nc.scalar.activation(out=first_silu[:], in_=ones_bf[:, 0:1], func=ACT.Silu)
        nc.vector.memset(base_scales[:].bitcast(I32), 0)

        turns = const.tile([P, NUM_F], F32)
        turns_late = const.tile([P, NUM_F], F32)
        period = const.tile([P, NUM_F], F32)
        minus_grid = const.tile([P, NUM_F], F32)
        coef_ps = psum.tile([P, PASSES, PACK, NUM_F], F32, tag="coef")
        w_codes = const.tile([P, UNITS, OUT_DIM], U32, align_bytes=64)
        w_scales = const.tile([P, UNITS, OUT_DIM], U8, align_bytes=64)
        base_sb = const.tile([P, SWEEPS * S_TILES, OUT_DIM], F32)
        gain_bc = const.tile([P, OUT_DIM], F32)
        bias_bc = const.tile([P, OUT_DIM], F32)
        x_ps = {}
        x_t = {}
        whole = {}
        frac = {}
        sine = {}
        s_bf = {}
        s_codes = {}
        s_scales = {}
        w_bf = {}
        silu = {}
        silu_codes = {}
        silu_scales = {}
        acc = {}
        scaled = {}
        last_base = {}

        def run_of_words(e):
            return slice(P * e, P * (e + 1))

        def every_second_word(e):
            return slice(e, 2 * P, 2)

        def where(v):
            h, u = divmod(v, UNITS)
            g, f = divmod(u, NUM_F)
            return h, u, g, f

        def transpose_x(h, g, bank, words):
            for e in range(2):
                for i in range(S_TILES):
                    nc.tensor.transpose(
                        bank[:, e, P * i : P * (i + 1)],
                        x_sb[h, g][:, i, :].bitcast(F32)[:, words(e)],
                        ident_f32[:],
                    )

        def x_to_psum(h, g):
            x_ps[h, g] = psum.tile([P, 2, SWEEP], F32, tag="x", name="x_ps")
            transpose_x(h, g, x_ps[h, g], run_of_words)

        def x_to_sbuf(h, g, bank):
            x_t[h, g] = const.tile([P, 2, SWEEP], F32, name="x_t_%d%d" % (h, g))
            nc.scalar.copy(out=x_t[h, g][:], in_=bank[:])

        def whole_turns(engine, v):
            h, u, g, f = where(v)
            whole[v] = five.tile([P, STEP], I32, align_bytes=64, name="whole", tag="gate")
            engine.tensor_scalar(
                out=whole[v][:],
                in0=x_t[h, g][:].rearrange("p e w -> p (e w)").bitcast(BF16),
                scalar1=(turns if v < 2 else turns_late)[:, f : f + 1],
                scalar2=0.0,
                op0=ALU.mult,
                op1=ALU.add,
            )

        def reduce_angle(v):
            h, u, g, f = where(v)
            frac[v] = five.tile([P, STEP], F32, name="frac", tag="frac")
            nc.vector.scalar_tensor_tensor(
                out=frac[v][:],
                in0=whole[v][:],
                scalar=period[:, f : f + 1],
                in1=x_ps[h, g][:].rearrange("p e w -> p (e w)").bitcast(BF16),
                op0=ALU.mult,
                op1=ALU.subtract,
            )

        def take_sine(v, i):
            if i == 0:
                sine[v] = four.tile([P, STEP], F32, name="sine", tag="sine")
            tokens = slice(P * i, P * (i + 1))
            angles = frac[v][:].rearrange("p (e w s) -> p e w s", e=2, s=2)[:, :, tokens, :]
            sines = sine[v][:].rearrange("p (w e s) -> p w e s", e=2, s=2)[:, tokens, :, :]
            angles = angles.rearrange("p e w s -> p w e s")
            f = v % NUM_F
            nc.scalar.activation(out=sines, in_=angles, func=ACT.Sin, scale=minus_grid[:, f : f + 1])

        def new_basis(v):
            s_bf[v] = five.tile([P, SWEEP, PACK], BF16, align_bytes=64, name="s_bf", tag="gate")

        def basis(v):
            h, u, g, f = where(v)
            mine = SWEEP - gpsimd_tokens(v)
            nc.vector.tensor_tensor(
                out=s_bf[v][:, 0:mine, :],
                in0=sine[v][:].rearrange("p (w t) -> p w t", t=PACK)[:, 0:mine, :],
                in1=coef_ps[:, g, :, f].unsqueeze(1).to_broadcast([P, mine, PACK]),
                op=ALU.mult,
            )

        def basis_by_gpsimd(v):
            h, u, g, f = where(v)
            n = gpsimd_tokens(v)
            nc.gpsimd.tensor_tensor(
                out=s_bf[v][:, SWEEP - n : SWEEP, :],
                in0=sine[v][:].rearrange("p (w t) -> p w t", t=PACK)[:, SWEEP - n : SWEEP, :],
                in1=coef_sb[:, g, :, f].unsqueeze(1).to_broadcast([P, n, PACK]),
                op=ALU.mult,
            )

        def quantise_basis(v):
            s_codes[v] = four.tile([P, SWEEP], U32, align_bytes=64, name="s_codes", tag="s_codes")
            s_scales[v] = four.tile([P, SWEEP], U8, align_bytes=64, name="s_scales", tag="s_scales")
            nc.vector.quantize_mx(
                out=s_codes[v][:].bitcast(FP8X4),
                scales=s_scales[v][:],
                in_=s_bf[v][:].rearrange("p w t -> p (w t)"),
            )

        def quantise_weights(u):
            for lo, hi in CHUNKS:
                nc.vector.quantize_mx(
                    out=w_codes[:, u, lo:hi].bitcast(FP8X4),
                    scales=w_scales[:, u, lo:hi],
                    in_=w_bf[u][:, lo:hi, :].rearrange("p o t -> p (o t)"),
                )

        def multiply(v, i):
            h, u, g, f = where(v)
            rows_i = slice(P * i, P * (i + 1))
            for c, (lo, hi) in enumerate(CHUNKS):
                nc.tensor.matmul_mx(
                    out=acc[h, i, c][:, 0 : hi - lo],
                    lhsT=s_codes[v][:, rows_i].bitcast(FP8X4),
                    lhsT_scale=s_scales[v][:, rows_i],
                    rhs=w_codes[:, u, lo:hi].bitcast(FP8X4),
                    rhs_scale=w_scales[:, u, lo:hi],
                    start=(u == 0),
                    stop=(u == UNITS - 1),
                )

        def keep_warm(v, bank):
            lo, hi = CHUNKS[0]
            nc.tensor.matmul_mx(
                out=bank,
                lhsT=s_codes[v][:, 0:P].bitcast(FP8X4),
                lhsT_scale=s_scales[v][:, 0:P],
                rhs=w_codes[:, v, lo:hi].bitcast(FP8X4),
                rhs_scale=w_scales[:, v, lo:hi],
                start=True,
                stop=True,
            )

        def weight_pair(u, jj):
            w_ps = psum_work.tile([P, 2, 2, P], F32, tag="work", name="w_ps")
            if jj == 0 and u >= 2 * WEIGHTS_AHEAD:
                keep_warm(u - 2 * WEIGHTS_AHEAD, w_ps[:].rearrange("p a e o -> p (a e o)"))
            for a in range(2):
                for e in range(2):
                    nc.tensor.transpose(
                        w_ps[:, a, e, :],
                        w_raw[u][:, 2 * jj + a, :].bitcast(F32)[:, run_of_words(e)],
                        ident_f32[:],
                    )
            nc.scalar.copy(
                out=w_bf[u][:, 2 * P * jj : 2 * P * (jj + 1), :].rearrange("p (a o) t -> p a o t", a=2).bitcast(F32),
                in_=w_ps[:].rearrange("p a e o -> p a o e"),
            )

        def new_weights(u):
            w_bf[u] = three.tile([P, OUT_DIM, PACK], BF16, align_bytes=64, name="w_bf", tag="w_bf")

        def stage_x(h, g):
            bank = psum_work.tile([P, 2, SWEEP], F32, tag="work", name="x_bank")
            transpose_x(h, g, bank, run_of_words)
            x_to_sbuf(h, g, bank)

        def take_silu(h, g):
            bank = psum_work.tile([P, 2, SWEEP], F32, tag="work", name="silu_bank")
            transpose_x(h, g, bank, every_second_word)
            silu[h, g] = two.tile([P, SWEEP, PACK], BF16, align_bytes=64, name="silu", tag="silu")
            nc.scalar.activation(
                out=silu[h, g][:].rearrange("p w (e s) -> p w e s", s=2),
                in_=bank[:].rearrange("p e w -> p (e w)").bitcast(BF16).rearrange("p (e w s) -> p w e s", e=2, s=2),
                func=ACT.Silu,
            )

        def quantise_silu(h, g):
            silu_codes[h, g] = const.tile([P, SWEEP], U32, align_bytes=64, name="silu_codes_%d%d" % (h, g))
            silu_scales[h, g] = const.tile([P, SWEEP], U8, align_bytes=64, name="silu_scales_%d%d" % (h, g))
            nc.vector.quantize_mx(
                out=silu_codes[h, g][:].bitcast(FP8X4),
                scales=silu_scales[h, g][:],
                in_=silu[h, g][:].rearrange("p w t -> p (w t)"),
            )

        def base_product(h, i, c):
            lo, hi = CHUNKS[c]
            rows_i = slice(P * i, P * (i + 1))
            bank = psum_work.tile([P, BANK], F32, tag="work", name="base_ps")
            for g in range(PASSES):
                nc.tensor.matmul_mx(
                    out=bank[:, 0 : hi - lo],
                    lhsT=silu_codes[h, g][:, rows_i].bitcast(FP8X4),
                    lhsT_scale=silu_scales[h, g][:, rows_i],
                    rhs=base_codes[:, g, lo:hi].bitcast(FP8X4),
                    rhs_scale=base_scales[:, g, lo:hi],
                    start=(g == 0),
                    stop=(g == PASSES - 1),
                )
            if (h, i) == LAST_TILE:
                last_base[c] = bank
            else:
                nc.scalar.copy(out=base_sb[:, S_TILES * h + i, lo:hi], in_=bank[:, 0 : hi - lo])

        def last_bias(c):
            lo, hi = CHUNKS[c]
            nc.vector.tensor_add(
                out=base_sb[:, SWEEPS * S_TILES - 1, lo:hi], in0=last_base[c][:, 0 : hi - lo], in1=bias_bc[:, lo:hi]
            )

        def add_bias(h, i, lo, hi):
            cols = base_sb[:, S_TILES * h + i, lo:hi]
            nc.gpsimd.tensor_tensor(out=cols, in0=cols, in1=bias_bc[:, lo:hi], op=ALU.add)

        def spread_row(r, c):
            lo, hi = CHUNKS[c]
            bank = psum_work.tile([P, BANK], F32, tag="work", name="row_ps")
            nc.tensor.matmul(
                out=bank[:, 0 : hi - lo], lhsT=ones_bf[:], rhs=rows[:, r, lo:hi], start=True, stop=True
            )
            return bank

        def spread_gain(c):
            lo, hi = CHUNKS[c]
            nc.scalar.copy(out=gain_bc[:, lo:hi], in_=spread_row(1, c)[:, 0 : hi - lo])

        def spread_bias(c):
            lo, hi = CHUNKS[c]
            nc.scalar.copy(out=bias_bc[:, lo:hi], in_=spread_row(0, c)[:, 0 : hi - lo])

        def scale_bias(n):
            cols = bias_bc[:, PIECE * n : PIECE * (n + 1)]
            nc.gpsimd.tensor_tensor(out=cols, in0=cols, in1=gain_bc[:, PIECE * n : PIECE * (n + 1)], op=ALU.mult)

        def scale_sums(h, i):
            scaled[h, i] = two.tile([P, OUT_DIM], F32, name="scaled", tag="scaled")
            for c, (lo, hi) in enumerate(CHUNKS):
                nc.vector.tensor_mul(
                    out=scaled[h, i][:, lo:hi], in0=acc[h, i, c][:, 0 : hi - lo], in1=gain_bc[:, lo:hi]
                )

        def add_base(engine, h, i, lo, hi, pool, tag):
            sums = pool.tile([P, hi - lo], F32, align_bytes=64, name="sums", tag=tag)
            engine.tensor_tensor(
                out=sums[:],
                in0=scaled[h, i][:, lo:hi],
                in1=base_sb[:, S_TILES * h + i, lo:hi],
                op=ALU.add,
            )
            row = P * (S_TILES * h + i)
            nc.sync.dma_start(out=outf[row : row + P, lo:hi], in_=sums[:])

        def new_accumulators(h):
            for i in range(S_TILES):
                for c in range(len(CHUNKS)):
                    acc[h, i, c] = psum.tile([P, BANK], F32, tag="acc%d%d" % (i, c), name="acc")

        nc.vector.tensor_scalar(
            out=turns[:], in0=grid_bc[:], scalar1=1.0 / (2.0 * math.pi), scalar2=None, op0=ALU.mult
        )
        nc.vector.tensor_scalar(out=period[:], in0=grid_bc[:], scalar1=0.0, scalar2=None, op0=ALU.is_equal)
        nc.vector.tensor_scalar(
            out=minus_grid[:], in0=grid_bc[:], scalar1=-1.0, scalar2=None, op0=ALU.mult
        )
        nc.vector.tensor_sub(out=period[:], in0=period[:], in1=minus_grid[:])
        nc.vector.reciprocal(out=period[:], in_=period[:])
        x_to_psum(0, 0)
        x_to_sbuf(0, 0, x_ps[0, 0])
        nc.tensor.matmul(
            out=coef_ps[:].rearrange("p g t f -> p (g t f)"),
            lhsT=ident_bf[:],
            rhs=coef_sb[:].rearrange("p g t f -> p (g t f)"),
            start=True,
            stop=True,
        )
        for v in range(2):
            whole_turns(nc.vector, v)
        nc.vector.tensor_scalar(
            out=period[:], in0=period[:], scalar1=2.0 * math.pi, scalar2=None, op0=ALU.mult
        )
        nc.vector.tensor_copy(out=turns_late[:], in_=turns[:])
        for c in range(len(CHUNKS)):
            spread_gain(c)
            spread_bias(c)
        for v in range(1, TURNS_AHEAD):
            if v >= ANGLES_AHEAD:
                new_basis(v - ANGLES_AHEAD)
            if v > 1:
                whole_turns(nc.gpsimd, v)
            if v <= ANGLES_AHEAD:
                reduce_angle(v - 1)
        for u in range(SINES_AHEAD):
            if u < WEIGHTS_AHEAD:
                new_weights(u)
                weight_pair(u, 0)
                weight_pair(u, 1)
            take_sine(u, 0)
            if u < WEIGHTS_AHEAD:
                weight_pair(u, 2)
                load_weights(u + 4)
            take_sine(u, 1)
        new_accumulators(0)

        extras = {}

        def at(step, call, *args):
            extras.setdefault(step, []).append((call, args))

        at(0, stage_x, 0, 1)
        for g in range(PASSES):
            at(13 + g, take_silu, 0, g)
            at(15 + g, quantise_silu, 0, g)
            at(2 + 2 * g, load_x, 1, g)
            at(7 + 8 * g, stage_x, 1, g)
            at(18 + g, take_silu, 1, g)
            at(21 + g, quantise_silu, 1, g)
        at(5, load_base)
        for n in range(3):
            at(6 + n, scale_bias, n)
        for i in range(S_TILES):
            for c in range(len(CHUNKS)):
                at(17 + i, base_product, 0, i, c)
                at(23 + i, base_product, 1, i, c)
            at(STEPS - 1, last_bias, i)
            for n in range(3):
                at(17 + 3 * i + n, add_bias, 0, i, PIECE * n, PIECE * (n + 1))
        at(23, add_base, nc.gpsimd, 0, 0, 0, 256, two, "sums_early")
        at(24, add_base, nc.gpsimd, 0, 0, 256, 512, two, "sums_early")
        at(25, add_base, nc.gpsimd, 0, 0, 512, 768, five, "gate")
        at(25, add_base, nc.gpsimd, 0, 1, 0, 512, two, "sums_512")
        at(26, add_base, nc.gpsimd, 0, 1, 512, 768, five, "gate")
        at(26, add_bias, 1, 0, 0, 512)
        at(27, add_bias, 1, 0, 512, 768)

        gpsimd_calls = (scale_bias, add_bias, add_base)

        def gpsimd_tokens(v):
            if v < 2 or any([call in gpsimd_calls for call, args in extras.get(v - 1, [])]):
                return 0
            return 32 if v < STEPS - 4 else 0

        for v in range(STEPS):
            h, u, g, f = where(v)
            ahead = v + ANGLES_AHEAD
            if ahead <= STEPS:
                basis(v)
            if ahead >= STEPS and v + 1 < STEPS:
                basis(v + 1)
            if ahead < STEPS:
                reduce_angle(ahead)
            if (ahead + 1) % NUM_F == 0 and ahead + 1 < STEPS:
                x_to_psum(*where(ahead + 1)[0::2])
            if h == 0:
                quantise_weights(u)
            quantise_basis(v)
            if v + BASIS_AHEAD < STEPS:
                new_basis(v + BASIS_AHEAD)
            if v + TURNS_AHEAD < STEPS:
                whole_turns(nc.gpsimd, v + TURNS_AHEAD)
            if v + 1 < STEPS and gpsimd_tokens(v + 1) > 0:
                basis_by_gpsimd(v + 1)
            new = v + WEIGHTS_AHEAD
            if new < UNITS:
                new_weights(new)
                weight_pair(new, 0)
                weight_pair(new, 1)
            if v > 0:
                multiply(v - 1, 0)
            if v + SINES_AHEAD < STEPS:
                take_sine(v + SINES_AHEAD, 0)
            if new < UNITS:
                weight_pair(new, 2)
            if v + SINES_AHEAD < STEPS:
                take_sine(v + SINES_AHEAD, 1)
            if new < UNITS:
                if v + 6 < UNITS:
                    load_weights(v + 6)
            if v > 0:
                multiply(v - 1, 1)
                if v == UNITS:
                    for i in range(S_TILES):
                        scale_sums(0, i)
                    new_accumulators(1)
            for call, args in extras.get(v, []):
                call(*args)
        for i in range(S_TILES):
            multiply(STEPS - 1, i)
        for i in range(S_TILES):
            scale_sums(1, i)
        for i in range(S_TILES):
            for c, (lo, hi) in enumerate(CHUNKS):
                add_base(nc.vector, 1, i, lo, hi, two, "sums_last%d" % c)
